import numpy as np
import ml_dtypes


def mxq(x, axis, fmt="e4m3"):
    dtype, down = {"e4m3": (ml_dtypes.float8_e4m3fn, 7), "e5m2": (ml_dtypes.float8_e5m2, 14)}[fmt]
    v = np.moveaxis(np.asarray(x, np.float32).astype(ml_dtypes.bfloat16).astype(np.float64), axis, -1)
    blocks = v.reshape(v.shape[:-1] + (-1, 32))
    amax = np.abs(blocks).max(-1, keepdims=True)
    byte = np.maximum(np.where(amax > 0, np.frexp(amax)[1] - 1 + 127, 0) - down, 1)
    scale = np.exp2(byte - 127.0)
    codes = (blocks / scale).astype(np.float32).astype(dtype).astype(np.float64)
    return np.moveaxis((codes * scale).reshape(v.shape), -1, axis)


WIDE = False


def mx_kscale(k):
    if not WIDE:
        return np.ones(k)
    levels = np.array([10, -10, 5, -5, 0])
    a = np.random.permutation(np.resize(levels, k // 512 * 4)).reshape(k // 512, 4)
    idx = np.arange(k)
    return np.exp2(a[idx // 512, idx % 128 // 32])


BF16 = ml_dtypes.bfloat16


def bf(x):
    return np.asarray(x, np.float32).astype(BF16)


def f64(x):
    return np.asarray(x).astype(np.float64)


B, L, H, K = 4, 64, 512, 128


def setup_inputs():
    u = np.exp2(np.round(np.log2(mx_kscale(H)) / 2))
    r = np.concatenate([u * u, u, u])
    return {"seq_out": bf(np.random.standard_normal((B, L, H)) * u),
            "W_proj": bf(np.random.standard_normal((3 * H, H)) * 0.5 / np.sqrt(H) / r[:, None]),
            "b_proj": bf(np.random.standard_normal(H) * 0.2),
            "W_out": bf(np.random.standard_normal((H, K)) * 1.5 / np.sqrt(H)),
            "b_out": bf(np.random.standard_normal(K) * 0.2)}


def reference(seq_out, W_proj, b_proj, W_out, b_out):
    x = f64(seq_out)
    W = f64(W_proj)
    W1, W2, W3 = W[:H], W[H:2 * H], W[2 * H:]
    p = x[:, :, None, :] * x[:, None, :, :]
    pw = mxq(p, 3, "e4m3") @ mxq(W1, 0, "e4m3")
    xq = mxq(x, 2, "e4m3")
    xi = (xq @ mxq(W2, 0, "e4m3"))[:, :, None, :]
    xj = (xq @ mxq(W3, 0, "e4m3"))[:, None, :, :]
    proj = np.tanh(pw + xi + xj + f64(b_proj))
    out = (mxq(proj, 3, "e4m3") @ mxq(f64(W_out), 0, "e4m3")) + f64(b_out)
    return out.transpose(0, 3, 1, 2)

@@ -1,0 +1,285 @@
+from contextlib import ExitStack
+
+import concourse.mybir as mybir
+from concourse.masks import make_identity
+
+FLOPS = 2 * 16384 * 512 * 512 + 2 * 2 * 256 * 512 * 512 + 2 * 16384 * 512 * 128
+
+BF16 = mybir.dt.bfloat16
+F32 = mybir.dt.float32
+U32 = mybir.dt.uint32
+U8 = mybir.dt.uint8
+I32 = mybir.dt.int32
+FP8X4 = mybir.dt.float8_e4m3fn_x4
+ACT = mybir.ActivationFunctionType
+ALU = mybir.AluOpType
+
+MANUAL = True
+
+P = 128
+B = 4
+L = 64
+H = 512
+T = 4
+TB = 16
+NB = L // TB
+BLK = TB * TB
+UNITS = B * NB * 2
+
+
+def regroup(engine_copy, dst, src):
+    engine_copy(
+        out=dst.rearrange("p (c i) t -> p c t i", i=4),
+        in_=src.rearrange("p t (c i) -> p c t i", i=4),
+    )
+
+
+def tile_srlbertold_pa_t_kernel(tc, seq_out, W_proj, b_proj, W_out, b_out, out):
+    nc = tc.nc
+    with ExitStack() as ctx:
+        if MANUAL:
+            ctx.enter_context(tc.manual_schedule())
+        keep = ctx.enter_context(tc.tile_pool(name="keep", bufs=1))
+        wstage = ctx.enter_context(tc.tile_pool(name="wstage", bufs=2))
+        pstage = ctx.enter_context(tc.tile_pool(name="pstage", bufs=4))
+        ring = ctx.enter_context(tc.tile_pool(name="ring", bufs=3))
+        ps1 = ctx.enter_context(tc.psum_pool(name="ps1", bufs=6))
+        ps2 = ctx.enter_context(tc.psum_pool(name="ps2", bufs=2))
+
+        x_sb = keep.tile([P, 2, H], BF16, name="x_sb")
+        nc.sync.dma_start(out=x_sb[:], in_=seq_out.rearrange("b l h -> (b l) h").rearrange("(g p) h -> p g h", p=P))
+        brows = keep.tile([P, P], BF16, name="brows")
+        nc.vector.memset(brows[:], 0.0)
+        nc.sync.dma_start(out=brows[0:4, :], in_=b_proj.rearrange("(t p) -> t p", p=P))
+        nc.sync.dma_start(out=brows[4:5, :], in_=b_out.rearrange("(o k) -> o k", o=1))
+        wraw = []
+        for w in range(3):
+            wr = keep.tile([P, T, H], BF16, name="wraw%d" % w)
+            nc.sync.dma_start(out=wr[:], in_=W_proj[H * w:H * (w + 1), :].rearrange("(t p) n -> p t n", p=P))
+            wraw.append(wr)
+        woraw = keep.tile([P, T, P], BF16, name="woraw")
+        nc.sync.dma_start(out=woraw[:], in_=W_out.rearrange("(t p) n -> p t n", p=P))
+
+        ident = keep.tile([P, P], BF16, name="ident")
+        make_identity(nc, ident[:])
+
+        warm = keep.tile([P, 1], F32, name="warm")
+        nc.vector.memset(warm[:], 0.0)
+        nc.scalar.activation(out=warm[:], in_=warm[:], func=ACT.Tanh)
+
+        xg = keep.tile([P, B * L, T], BF16, name="xg", align_bytes=64)
+        xc = keep.tile([P, B * L], U32, name="xc", align_bytes=64)
+        xs = keep.tile([P, B * L], U8, name="xs", align_bytes=64)
+        x4c = keep.tile([P, B * L * 4], U32, name="x4c", align_bytes=64)
+        x4s = keep.tile([P, B * L * 4], U8, name="x4s", align_bytes=64)
+        xfc = keep.tile([P, B * L * TB], U32, name="xfc", align_bytes=64)
+        xfs = keep.tile([P, B * L * TB], U8, name="xfs", align_bytes=64)
+        xsc = keep.tile([P, B * L * TB], U32, name="xsc", align_bytes=64)
+        xss = keep.tile([P, B * L * TB], U8, name="xss", align_bytes=64)
+        nc.vector.memset(xs[:].bitcast(I32), 0)
+        nc.vector.memset(x4s[:].bitcast(I32), 0)
+        wc = [keep.tile([P, H], U32, name="wc%d" % w, align_bytes=64) for w in range(3)]
+        ws = [keep.tile([P, H], U8, name="ws%d" % w, align_bytes=64) for w in range(3)]
+        woc = keep.tile([P, P], U32, name="woc", align_bytes=64)
+        wos = keep.tile([P, P], U8, name="wos", align_bytes=64)
+        NPB = NB * (NB + 1) // 2
+        pc = keep.tile([P, B * NPB, BLK], U32, name="pc", align_bytes=64)
+        psc = keep.tile([P, B * NPB, BLK], U8, name="psc", align_bytes=64)
+        biasf = keep.tile([P, 8], F32, name="biasf")
+
+        for g in range(2):
+            xt = ps2.tile([P, T, P], BF16, name="xt", tag="s2")
+            for t in range(T):
+                nc.tensor.transpose(xt[:, t, :], x_sb[:, g, P * t:P * (t + 1)], ident[:])
+            nc.vector.tensor_copy(out=xg[:, P * g:P * (g + 1), :], in_=xt[:].rearrange("p t r -> p r t"))
+        bps = ps1.tile([P, P], BF16, name="bps", tag="s1")
+        nc.tensor.transpose(bps[:], brows[:], ident[:])
+        nc.vector.tensor_copy(out=biasf[:], in_=bps[:, 0:8])
+
+        def quant_x(g):
+            nc.vector.quantize_mx(
+                out=xc[:, P * g:P * (g + 1)].bitcast(FP8X4),
+                scales=xs[:, P * g:P * (g + 1)],
+                in_=xg[:, P * g:P * (g + 1), :].rearrange("p r t -> p (r t)"),
+            )
+
+        def x_rep_a(b):
+            x4 = wstage.tile([P, L, 4, T], BF16, name="x4", tag="x4", align_bytes=64)
+            nc.vector.tensor_copy(out=x4[:], in_=xg[:, L * b:L * (b + 1), :].unsqueeze(2).to_broadcast([P, L, 4, T]))
+            return x4
+
+        def x_rep_b(b, x4):
+            nc.vector.quantize_mx(
+                out=x4c[:, 4 * L * b:4 * L * (b + 1)].bitcast(FP8X4),
+                scales=x4s[:, 4 * L * b:4 * L * (b + 1)],
+                in_=x4[:].rearrange("p r q t -> p (r q t)"),
+            )
+
+        def x_rep_c(b):
+            n = L * TB
+            nc.vector.tensor_copy(
+                out=xfc[:, n * b:n * (b + 1)].bitcast(I32).rearrange("p (r q) -> p r q", q=TB),
+                in_=xc[:, L * b:L * (b + 1)].bitcast(I32).unsqueeze(2).to_broadcast([P, L, TB]),
+            )
+            nc.vector.tensor_copy(
+                out=xsc[:, n * b:n * (b + 1)].bitcast(I32).rearrange("p (c q j) -> p c q j", q=TB, j=TB),
+                in_=xc[:, L * b:L * (b + 1)].bitcast(I32).rearrange("p (c j) -> p c j", j=TB).unsqueeze(2).to_broadcast([P, NB, TB, TB]),
+            )
+            nc.vector.tensor_copy(
+                out=xfs[:, n * b:n * (b + 1)].bitcast(I32).rearrange("p (r q) -> p r q", q=TB // 4),
+                in_=x4s[:, 4 * L * b:4 * L * (b + 1)].bitcast(I32).unsqueeze(2).to_broadcast([P, L, TB // 4]),
+            )
+            nc.vector.tensor_copy(
+                out=xss[:, n * b:n * (b + 1)].bitcast(I32).rearrange("p (c q j) -> p c q j", q=TB, j=TB // 4),
+                in_=xs[:, L * b:L * (b + 1)].bitcast(I32).rearrange("p (c j) -> p c j", j=TB // 4).unsqueeze(2).to_broadcast([P, NB, TB, TB // 4]),
+            )
+
+        pidx = {}
+        porder = []
+        for b in range(B):
+            for a in range(NB):
+                for c in range(a, NB):
+                    pidx[(b, a, c)] = len(porder)
+                    porder.append((b, a, c))
+
+        def p_mul(i):
+            b, a, c = porder[i]
+            pb = pstage.tile([P, TB, TB, T], BF16, name="pb", tag="pb", align_bytes=64)
+            ta = L * b + TB * a
+            tcc = L * b + TB * c
+            nc.vector.tensor_tensor(
+                out=pb[:],
+                in0=xg[:, ta:ta + TB, :].unsqueeze(2).to_broadcast([P, TB, TB, T]),
+                in1=xg[:, tcc:tcc + TB, :].unsqueeze(1).to_broadcast([P, TB, TB, T]),
+                op=ALU.mult,
+            )
+            return pb
+
+        def p_quant(i, pb):
+            nc.vector.quantize_mx(
+                out=pc[:, i, :].bitcast(FP8X4),
+                scales=psc[:, i, :],
+                in_=pb[:].rearrange("p i j t -> p (i j t)"),
+            )
+
+        def w_regroup(copy_fn, w):
+            wg = wstage.tile([P, H, T], BF16, name="wg", tag="wg", align_bytes=64, bufs=3)
+            regroup(copy_fn, wg[:], wraw[w][:])
+            return wg
+
+        def w_quant(w, wg):
+            nc.vector.quantize_mx(out=wc[w][:].bitcast(FP8X4), scales=ws[w][:], in_=wg[:].rearrange("p n t -> p (n t)"))
+
+        wg1 = w_regroup(nc.scalar.copy, 1)
+        wg0 = w_regroup(nc.vector.tensor_copy, 0)
+        quant_x(0)
+        pb0 = p_mul(0)
+        w_quant(0, wg0)
+        x40 = x_rep_a(0)
+        p_quant(0, pb0)
+        pb1 = p_mul(1)
+        x_rep_b(0, x40)
+        wg2 = w_regroup(nc.vector.tensor_copy, 2)
+        w_quant(1, wg1)
+        x_rep_c(0)
+        w_quant(2, wg2)
+        p_quant(1, pb1)
+        pb2 = p_mul(2)
+        pb3 = p_mul(3)
+        quant_x(1)
+        p_quant(2, pb2)
+        p_quant(3, pb3)
+        wog = wstage.tile([P, P, T], BF16, name="wog", tag="wog", align_bytes=64, bufs=1)
+        regroup(nc.scalar.copy, wog[:], woraw[:])
+        nc.vector.quantize_mx(out=woc[:].bitcast(FP8X4), scales=wos[:], in_=wog[:].rearrange("p n t -> p (n t)"))
+
+        need = []
+        cnt = 0
+        for u in range(UNITS):
+            a = (u // 2) % NB
+            for c in (2 * (u % 2), 2 * (u % 2) + 1):
+                if c >= a:
+                    cnt += 1
+            need.append(cnt)
+
+        def stage1(u, t, pl):
+            b, a, hh = u // (2 * NB), (u // 2) % NB, u % 2
+            bank = ps1.tile([P, 2 * BLK], F32, name="bank", tag="s1")
+            hs = slice(P * t, P * (t + 1))
+            for e in range(2):
+                c = 2 * hh + e
+                o = bank[:, BLK * e:BLK * (e + 1)]
+                i = pidx[(b, min(a, c), max(a, c))]
+                sa = slice(BLK * (NB * b + a), BLK * (NB * b + a + 1))
+                scc = slice(BLK * (NB * b + c), BLK * (NB * b + c + 1))
+                if a <= c:
+                    first_c, first_s, second_c, second_s = xfc, xfs, xsc, xss
+                else:
+                    first_c, first_s, second_c, second_s = xsc, xss, xfc, xfs
+                nc.tensor.matmul_mx(out=o, lhsT=wc[0][:, hs].bitcast(FP8X4), lhsT_scale=ws[0][:, hs],
+                                    rhs=pc[:, i, :].bitcast(FP8X4), rhs_scale=psc[:, i, :], start=True, stop=False)
+                nc.tensor.matmul_mx(out=o, lhsT=wc[1][:, hs].bitcast(FP8X4), lhsT_scale=ws[1][:, hs],
+                                    rhs=first_c[:, sa].bitcast(FP8X4), rhs_scale=first_s[:, sa], start=False, stop=False)
+                nc.tensor.matmul_mx(out=o, lhsT=wc[2][:, hs].bitcast(FP8X4), lhsT_scale=ws[2][:, hs],
+                                    rhs=second_c[:, scc].bitcast(FP8X4), rhs_scale=second_s[:, scc], start=False, stop=True)
+            nc.scalar.activation(out=pl[:, t, :], in_=bank[:], func=ACT.Tanh, bias=biasf[:, t:t + 1], scale=1.0)
+
+        planes = {}
+        grouped = {}
+        codes = {}
+        ostage = {}
+        pending = []
+        done_mul = 4
+
+        for s in range(UNITS + 2):
+            u2 = s - 2
+            if u2 >= 0:
+                b, a, hh = u2 // (2 * NB), (u2 // 2) % NB, u2 % 2
+                qc, qs = codes[u2]
+                bank2 = ps2.tile([P, 2 * BLK], F32, name="bank2", tag="s2")
+                nc.tensor.matmul_mx(out=bank2[:], lhsT=woc[:].bitcast(FP8X4), lhsT_scale=wos[:],
+                                    rhs=qc[:].bitcast(FP8X4), rhs_scale=qs[:], start=True, stop=True)
+                if hh == 0:
+                    ost = ring.tile([P, TB, L], F32, name="ost", tag="ost")
+                    ostage[(b, a)] = ost
+                ost = ostage[(b, a)]
+                for e in range(2):
+                    c = 2 * hh + e
+                    src = bank2[:, BLK * e:BLK * (e + 1)]
+                    if a <= c:
+                        view = src.rearrange("p (f s) -> p f s", f=TB)
+                    else:
+                        view = src.rearrange("p (s f) -> p f s", s=TB)
+                    nc.scalar.activation(out=ost[:, :, TB * c:TB * (c + 1)], in_=view, func=ACT.Identity,
+                                         bias=biasf[:, 4:5], scale=1.0)
+                if hh == 1:
+                    nc.sync.dma_start(out=out[b, :, TB * a:TB * (a + 1), :].rearrange("k f s -> k (f s)"),
+                                      in_=ost[:].rearrange("p f s -> p (f s)"))
+            if s < UNITS:
+                pl = ring.tile([P, T, 2 * BLK], BF16, name="pl", tag="pl")
+                planes[s] = pl
+                for t in range(T):
+                    stage1(s, t, pl)
+            u1 = s - 1
+            if 0 <= u1 < UNITS:
+                g2 = ring.tile([P, 2 * BLK, T], BF16, name="g2", tag="g2", align_bytes=64)
+                regroup(nc.vector.tensor_copy, g2[:], planes[u1][:])
+            for i, pb in pending:
+                p_quant(i, pb)
+            pending = []
+            if 0 <= u1 < UNITS:
+                qc = ring.tile([P, 2 * BLK], U32, name="qc", tag="qc", align_bytes=64)
+                qs = ring.tile([P, 2 * BLK], U8, name="qs", tag="qs", align_bytes=64)
+                nc.vector.quantize_mx(out=qc[:].bitcast(FP8X4), scales=qs[:], in_=g2[:].rearrange("p n t -> p (n t)"))
+                codes[u1] = (qc, qs)
+            target = min(len(porder), max(need[min(s + 2, UNITS - 1)], (5 * (s + 4) + 3) // 4))
+            while done_mul < target:
+                pending.append((done_mul, p_mul(done_mul)))
+                done_mul += 1
+            if s % (2 * NB) == 2 and s // (2 * NB) + 1 < B:
+                nb = s // (2 * NB) + 1
+                x4n = x_rep_a(nb)
+            if s % (2 * NB) == 3 and s // (2 * NB) + 1 < B:
+                x_rep_b(s // (2 * NB) + 1, x4n)
+            if s % (2 * NB) == 4 and s // (2 * NB) + 1 < B:
+                x_rep_c(s // (2 * NB) + 1)

@@ -24,6 +24,8 @@ T = 4
 TB = 16
 NB = L // TB
 BLK = TB * TB
+LAGD = 3
+PLEAD = 4
 UNITS = B * NB * 2
 
 
@@ -40,8 +42,6 @@ def tile_srlbertold_pa_t_kernel(tc, seq_out, W_proj, b_proj, W_out, b_out, out):
         if MANUAL:
             ctx.enter_context(tc.manual_schedule())
         keep = ctx.enter_context(tc.tile_pool(name="keep", bufs=1))
-        wstage = ctx.enter_context(tc.tile_pool(name="wstage", bufs=2))
-        pstage = ctx.enter_context(tc.tile_pool(name="pstage", bufs=4))
         ring = ctx.enter_context(tc.tile_pool(name="ring", bufs=3))
         ps1 = ctx.enter_context(tc.psum_pool(name="ps1", bufs=6))
         ps2 = ctx.enter_context(tc.psum_pool(name="ps2", bufs=2))
@@ -50,13 +50,14 @@ def tile_srlbertold_pa_t_kernel(tc, seq_out, W_proj, b_proj, W_out, b_out, out):
         nc.sync.dma_start(out=x_sb[:], in_=seq_out.rearrange("b l h -> (b l) h").rearrange("(g p) h -> p g h", p=P))
         brows = keep.tile([P, P], BF16, name="brows")
         nc.vector.memset(brows[:], 0.0)
-        nc.sync.dma_start(out=brows[0:4, :], in_=b_proj.rearrange("(t p) -> t p", p=P))
-        nc.sync.dma_start(out=brows[4:5, :], in_=b_out.rearrange("(o k) -> o k", o=1))
         wraw = []
         for w in range(3):
             wr = keep.tile([P, T, H], BF16, name="wraw%d" % w)
             nc.sync.dma_start(out=wr[:], in_=W_proj[H * w:H * (w + 1), :].rearrange("(t p) n -> p t n", p=P))
             wraw.append(wr)
+            if w == 0:
+                nc.sync.dma_start(out=brows[0:4, :], in_=b_proj.rearrange("(t p) -> t p", p=P))
+                nc.sync.dma_start(out=brows[4:5, :], in_=b_out.rearrange("(o k) -> o k", o=1))
         woraw = keep.tile([P, T, P], BF16, name="woraw")
         nc.sync.dma_start(out=woraw[:], in_=W_out.rearrange("(t p) n -> p t n", p=P))
 
@@ -78,6 +79,7 @@ def tile_srlbertold_pa_t_kernel(tc, seq_out, W_proj, b_proj, W_out, b_out, out):
         xss = keep.tile([P, B * L * TB], U8, name="xss", align_bytes=64)
         nc.vector.memset(xs[:].bitcast(I32), 0)
         nc.vector.memset(x4s[:].bitcast(I32), 0)
+        wg = [keep.tile([P, H, T], BF16, name="wg%d" % w, align_bytes=64) for w in range(3)]
         wc = [keep.tile([P, H], U32, name="wc%d" % w, align_bytes=64) for w in range(3)]
         ws = [keep.tile([P, H], U8, name="ws%d" % w, align_bytes=64) for w in range(3)]
         woc = keep.tile([P, P], U32, name="woc", align_bytes=64)
@@ -87,14 +89,11 @@ def tile_srlbertold_pa_t_kernel(tc, seq_out, W_proj, b_proj, W_out, b_out, out):
         psc = keep.tile([P, B * NPB, BLK], U8, name="psc", align_bytes=64)
         biasf = keep.tile([P, 8], F32, name="biasf")
 
-        for g in range(2):
+        def x_transpose(g):
             xt = ps2.tile([P, T, P], BF16, name="xt", tag="s2")
             for t in range(T):
                 nc.tensor.transpose(xt[:, t, :], x_sb[:, g, P * t:P * (t + 1)], ident[:])
             nc.vector.tensor_copy(out=xg[:, P * g:P * (g + 1), :], in_=xt[:].rearrange("p t r -> p r t"))
-        bps = ps1.tile([P, P], BF16, name="bps", tag="s1")
-        nc.tensor.transpose(bps[:], brows[:], ident[:])
-        nc.vector.tensor_copy(out=biasf[:], in_=bps[:, 0:8])
 
         def quant_x(g):
             nc.vector.quantize_mx(
@@ -104,7 +103,7 @@ def tile_srlbertold_pa_t_kernel(tc, seq_out, W_proj, b_proj, W_out, b_out, out):
             )
 
         def x_rep_a(b):
-            x4 = wstage.tile([P, L, 4, T], BF16, name="x4", tag="x4", align_bytes=64)
+            x4 = ring.tile([P, L, 4, T], BF16, name="x4", tag="x4", align_bytes=64, bufs=2)
             nc.vector.tensor_copy(out=x4[:], in_=xg[:, L * b:L * (b + 1), :].unsqueeze(2).to_broadcast([P, L, 4, T]))
             return x4
 
@@ -115,92 +114,100 @@ def tile_srlbertold_pa_t_kernel(tc, seq_out, W_proj, b_proj, W_out, b_out, out):
                 in_=x4[:].rearrange("p r q t -> p (r q t)"),
             )
 
-        def x_rep_c(b):
-            n = L * TB
+        NX = L * TB
+
+        def x_rep_words(b):
             nc.vector.tensor_copy(
-                out=xfc[:, n * b:n * (b + 1)].bitcast(I32).rearrange("p (r q) -> p r q", q=TB),
+                out=xfc[:, NX * b:NX * (b + 1)].bitcast(I32).rearrange("p (r q) -> p r q", q=TB),
                 in_=xc[:, L * b:L * (b + 1)].bitcast(I32).unsqueeze(2).to_broadcast([P, L, TB]),
             )
             nc.vector.tensor_copy(
-                out=xsc[:, n * b:n * (b + 1)].bitcast(I32).rearrange("p (c q j) -> p c q j", q=TB, j=TB),
+                out=xsc[:, NX * b:NX * (b + 1)].bitcast(I32).rearrange("p (c q j) -> p c q j", q=TB, j=TB),
                 in_=xc[:, L * b:L * (b + 1)].bitcast(I32).rearrange("p (c j) -> p c j", j=TB).unsqueeze(2).to_broadcast([P, NB, TB, TB]),
             )
+
+        def x_rep_scales(b):
             nc.vector.tensor_copy(
-                out=xfs[:, n * b:n * (b + 1)].bitcast(I32).rearrange("p (r q) -> p r q", q=TB // 4),
+                out=xfs[:, NX * b:NX * (b + 1)].bitcast(I32).rearrange("p (r q) -> p r q", q=TB // 4),
                 in_=x4s[:, 4 * L * b:4 * L * (b + 1)].bitcast(I32).unsqueeze(2).to_broadcast([P, L, TB // 4]),
             )
             nc.vector.tensor_copy(
-                out=xss[:, n * b:n * (b + 1)].bitcast(I32).rearrange("p (c q j) -> p c q j", q=TB, j=TB // 4),
+                out=xss[:, NX * b:NX * (b + 1)].bitcast(I32).rearrange("p (c q j) -> p c q j", q=TB, j=TB // 4),
                 in_=xs[:, L * b:L * (b + 1)].bitcast(I32).rearrange("p (c j) -> p c j", j=TB // 4).unsqueeze(2).to_broadcast([P, NB, TB, TB // 4]),
             )
 
         pidx = {}
-        porder = []
         for b in range(B):
             for a in range(NB):
                 for c in range(a, NB):
-                    pidx[(b, a, c)] = len(porder)
-                    porder.append((b, a, c))
+                    pidx[(b, a, c)] = len(pidx)
 
-        def p_mul(i):
-            b, a, c = porder[i]
-            pb = pstage.tile([P, TB, TB, T], BF16, name="pb", tag="pb", align_bytes=64)
+        def p_mul(b, a, c0, c1):
+            n = c1 - c0
+            pb = ring.tile([P, n, TB, TB, T], BF16, name="pb", tag="pb", align_bytes=64, bufs=3)
             ta = L * b + TB * a
-            tcc = L * b + TB * c
-            nc.vector.tensor_tensor(
-                out=pb[:],
-                in0=xg[:, ta:ta + TB, :].unsqueeze(2).to_broadcast([P, TB, TB, T]),
-                in1=xg[:, tcc:tcc + TB, :].unsqueeze(1).to_broadcast([P, TB, TB, T]),
-                op=ALU.mult,
-            )
-            return pb
+            tcc = L * b + TB * c0
+            for k in range(n):
+                nc.vector.tensor_tensor(
+                    out=pb[:, k],
+                    in0=xg[:, ta:ta + TB, :].unsqueeze(2).to_broadcast([P, TB, TB, T]),
+                    in1=xg[:, tcc + TB * k:tcc + TB * (k + 1), :].unsqueeze(1).to_broadcast([P, TB, TB, T]),
+                    op=ALU.mult,
+                )
+            return (b, a, c0, c1, pb)
 
-        def p_quant(i, pb):
-            nc.vector.quantize_mx(
-                out=pc[:, i, :].bitcast(FP8X4),
-                scales=psc[:, i, :],
-                in_=pb[:].rearrange("p i j t -> p (i j t)"),
-            )
+        def p_quant(job):
+            b, a, c0, c1, pb = job
+            c = c0
+            while c < c1:
+                n = 4 if c1 - c >= 4 else (2 if c1 - c >= 2 else 1)
+                i = pidx[(b, a, c)]
+                nc.vector.quantize_mx(
+                    out=pc[:, i:i + n, :].rearrange("p n w -> p (n w)").bitcast(FP8X4),
+                    scales=psc[:, i:i + n, :].rearrange("p n w -> p (n w)"),
+                    in_=pb[:, c - c0:c - c0 + n].rearrange("p c i j t -> p (c i j t)"),
+                )
+                c += n
 
-        def w_regroup(copy_fn, w):
-            wg = wstage.tile([P, H, T], BF16, name="wg", tag="wg", align_bytes=64, bufs=3)
-            regroup(copy_fn, wg[:], wraw[w][:])
-            return wg
+        def w_regroup(copy_fn, w, n0, n1):
+            regroup(copy_fn, wg[w][:, n0:n1, :], wraw[w][:, :, n0:n1])
 
-        def w_quant(w, wg):
-            nc.vector.quantize_mx(out=wc[w][:].bitcast(FP8X4), scales=ws[w][:], in_=wg[:].rearrange("p n t -> p (n t)"))
+        def w_quant(w, n0, n1):
+            nc.vector.quantize_mx(out=wc[w][:, n0:n1].bitcast(FP8X4), scales=ws[w][:, n0:n1],
+                                  in_=wg[w][:, n0:n1, :].rearrange("p n t -> p (n t)"))
 
-        wg1 = w_regroup(nc.scalar.copy, 1)
-        wg0 = w_regroup(nc.vector.tensor_copy, 0)
+        x_transpose(0)
         quant_x(0)
-        pb0 = p_mul(0)
-        w_quant(0, wg0)
+        job0 = p_mul(0, 0, 0, 2)
+        w_regroup(nc.vector.tensor_copy, 0, 0, P)
+        w_regroup(nc.scalar.copy, 1, 0, P)
         x40 = x_rep_a(0)
-        p_quant(0, pb0)
-        pb1 = p_mul(1)
+        p_quant(job0)
+        w_quant(0, 0, P)
         x_rep_b(0, x40)
-        wg2 = w_regroup(nc.vector.tensor_copy, 2)
-        w_quant(1, wg1)
-        x_rep_c(0)
-        w_quant(2, wg2)
-        p_quant(1, pb1)
-        pb2 = p_mul(2)
-        pb3 = p_mul(3)
+        w_regroup(nc.vector.tensor_copy, 2, 0, P)
+        x_rep_words(0)
+        w_quant(1, 0, P)
+        x_rep_scales(0)
+        w_quant(2, 0, P)
+        bps = ps1.tile([P, P], BF16, name="bps", tag="s1")
+        nc.tensor.transpose(bps[:], brows[:], ident[:])
+        nc.vector.tensor_copy(out=biasf[:], in_=bps[:, 0:8])
+        for n0, n1 in ((P, 2 * P), (2 * P, H)):
+            w_regroup(nc.scalar.copy, 1, n0, n1)
+            w_regroup(nc.vector.tensor_copy, 0, n0, n1)
+            w_regroup(nc.vector.tensor_copy, 2, n0, n1)
+            for w in range(3):
+                w_quant(w, n0, n1)
+        job1 = p_mul(0, 0, 2, 4)
+        x_transpose(1)
+        p_quant(job1)
+        job2 = p_mul(0, 1, 1, 4)
         quant_x(1)
-        p_quant(2, pb2)
-        p_quant(3, pb3)
-        wog = wstage.tile([P, P, T], BF16, name="wog", tag="wog", align_bytes=64, bufs=1)
+        p_quant(job2)
+        wog = keep.tile([P, P, T], BF16, name="wog", align_bytes=64)
         regroup(nc.scalar.copy, wog[:], woraw[:])
         nc.vector.quantize_mx(out=woc[:].bitcast(FP8X4), scales=wos[:], in_=wog[:].rearrange("p n t -> p (n t)"))
-
-        need = []
-        cnt = 0
-        for u in range(UNITS):
-            a = (u // 2) % NB
-            for c in (2 * (u % 2), 2 * (u % 2) + 1):
-                if c >= a:
-                    cnt += 1
-            need.append(cnt)
 
         def stage1(u, t, pl):
             b, a, hh = u // (2 * NB), (u // 2) % NB, u % 2
@@ -224,62 +231,66 @@ def tile_srlbertold_pa_t_kernel(tc, seq_out, W_proj, b_proj, W_out, b_out, out):
                                     rhs=second_c[:, scc].bitcast(FP8X4), rhs_scale=second_s[:, scc], start=False, stop=True)
             nc.scalar.activation(out=pl[:, t, :], in_=bank[:], func=ACT.Tanh, bias=biasf[:, t:t + 1], scale=1.0)
 
+        def stage2(u, qc, qs, ost):
+            b, a, hh = u // (2 * NB), (u // 2) % NB, u % 2
+            bank2 = ps2.tile([P, 2 * BLK], F32, name="bank2", tag="s2")
+            nc.tensor.matmul_mx(out=bank2[:], lhsT=woc[:].bitcast(FP8X4), lhsT_scale=wos[:],
+                                rhs=qc[:].bitcast(FP8X4), rhs_scale=qs[:], start=True, stop=True)
+            c = 2 * hh
+            if a <= c or a > c + 1:
+                if a <= c:
+                    view = bank2[:].rearrange("p (e f s) -> p f e s", e=2, f=TB)
+                else:
+                    view = bank2[:].rearrange("p (e s f) -> p f e s", e=2, s=TB)
+                nc.scalar.activation(out=ost[:, :, TB * c:TB * (c + 2)].rearrange("p f (e s) -> p f e s", e=2),
+                                     in_=view, func=ACT.Identity, bias=biasf[:, 4:5], scale=1.0)
+            else:
+                nc.scalar.activation(out=ost[:, :, TB * c:TB * (c + 1)],
+                                     in_=bank2[:, 0:BLK].rearrange("p (s f) -> p f s", s=TB),
+                                     func=ACT.Identity, bias=biasf[:, 4:5], scale=1.0)
+                nc.scalar.activation(out=ost[:, :, TB * (c + 1):TB * (c + 2)],
+                                     in_=bank2[:, BLK:2 * BLK].rearrange("p (f s) -> p f s", f=TB),
+                                     func=ACT.Identity, bias=biasf[:, 4:5], scale=1.0)
+            if hh == 1:
+                nc.sync.dma_start(out=out[b, :, TB * a:TB * (a + 1), :].rearrange("k f s -> k (f s)"),
+                                  in_=ost[:].rearrange("p f s -> p (f s)"))
+
         planes = {}
-        grouped = {}
         codes = {}
         ostage = {}
         pending = []
-        done_mul = 4
-
-        for s in range(UNITS + 2):
-            u2 = s - 2
+        x4n = x40
+        for s in range(UNITS + LAGD):
+            u2 = s - LAGD
             if u2 >= 0:
-                b, a, hh = u2 // (2 * NB), (u2 // 2) % NB, u2 % 2
-                qc, qs = codes[u2]
-                bank2 = ps2.tile([P, 2 * BLK], F32, name="bank2", tag="s2")
-                nc.tensor.matmul_mx(out=bank2[:], lhsT=woc[:].bitcast(FP8X4), lhsT_scale=wos[:],
-                                    rhs=qc[:].bitcast(FP8X4), rhs_scale=qs[:], start=True, stop=True)
-                if hh == 0:
-                    ost = ring.tile([P, TB, L], F32, name="ost", tag="ost")
-                    ostage[(b, a)] = ost
-                ost = ostage[(b, a)]
-                for e in range(2):
-                    c = 2 * hh + e
-                    src = bank2[:, BLK * e:BLK * (e + 1)]
-                    if a <= c:
-                        view = src.rearrange("p (f s) -> p f s", f=TB)
-                    else:
-                        view = src.rearrange("p (s f) -> p f s", s=TB)
-                    nc.scalar.activation(out=ost[:, :, TB * c:TB * (c + 1)], in_=view, func=ACT.Identity,
-                                         bias=biasf[:, 4:5], scale=1.0)
-                if hh == 1:
-                    nc.sync.dma_start(out=out[b, :, TB * a:TB * (a + 1), :].rearrange("k f s -> k (f s)"),
-                                      in_=ost[:].rearrange("p f s -> p (f s)"))
+                if u2 % 2 == 0:
+                    ostage[u2 // 2] = ring.tile([P, TB, L], F32, name="ost", tag="ost", bufs=3)
+                stage2(u2, codes[u2][0], codes[u2][1], ostage[u2 // 2])
             if s < UNITS:
-                pl = ring.tile([P, T, 2 * BLK], BF16, name="pl", tag="pl")
-                planes[s] = pl
+                planes[s] = ring.tile([P, T, 2 * BLK], BF16, name="pl", tag="pl", bufs=4)
                 for t in range(T):
-                    stage1(s, t, pl)
+                    stage1(s, t, planes[s])
             u1 = s - 1
             if 0 <= u1 < UNITS:
-                g2 = ring.tile([P, 2 * BLK, T], BF16, name="g2", tag="g2", align_bytes=64)
+                g2 = ring.tile([P, 2 * BLK, T], BF16, name="g2", tag="g2", align_bytes=64, bufs=3)
                 regroup(nc.vector.tensor_copy, g2[:], planes[u1][:])
-            for i, pb in pending:
-                p_quant(i, pb)
+            for job in pending:
+                p_quant(job)
             pending = []
             if 0 <= u1 < UNITS:
-                qc = ring.tile([P, 2 * BLK], U32, name="qc", tag="qc", align_bytes=64)
-                qs = ring.tile([P, 2 * BLK], U8, name="qs", tag="qs", align_bytes=64)
+                qc = ring.tile([P, 2 * BLK], U32, name="qc", tag="qc", align_bytes=64, bufs=LAGD + 2)
+                qs = ring.tile([P, 2 * BLK], U8, name="qs", tag="qs", align_bytes=64, bufs=LAGD + 2)
                 nc.vector.quantize_mx(out=qc[:].bitcast(FP8X4), scales=qs[:], in_=g2[:].rearrange("p n t -> p (n t)"))
                 codes[u1] = (qc, qs)
-            target = min(len(porder), max(need[min(s + 2, UNITS - 1)], (5 * (s + 4) + 3) // 4))
-            while done_mul < target:
-                pending.append((done_mul, p_mul(done_mul)))
-                done_mul += 1
-            if s % (2 * NB) == 2 and s // (2 * NB) + 1 < B:
-                nb = s // (2 * NB) + 1
-                x4n = x_rep_a(nb)
-            if s % (2 * NB) == 3 and s // (2 * NB) + 1 < B:
-                x_rep_b(s // (2 * NB) + 1, x4n)
-            if s % (2 * NB) == 4 and s // (2 * NB) + 1 < B:
-                x_rep_c(s // (2 * NB) + 1)
+            r = s + PLEAD
+            if r % 2 == 0 and r < UNITS:
+                pending.append(p_mul(r // (2 * NB), (r // 2) % NB, (r // 2) % NB, NB))
+            nb = s // (2 * NB) + 1
+            if nb < B:
+                if s % (2 * NB) == 1:
+                    x4n = x_rep_a(nb)
+                    x_rep_words(nb)
+                if s % (2 * NB) == 3:
+                    x_rep_b(nb, x4n)
+                if s % (2 * NB) == 5:
+                    x_rep_scales(nb)

@@ -26,6 +26,7 @@ NB = L // TB
 BLK = TB * TB
 LAGD = 3
 PLEAD = 4
+ECHUNKS = (1, 3)
 UNITS = B * NB * 2
 
 
@@ -88,6 +89,7 @@ def tile_srlbertold_pa_t_kernel(tc, seq_out, W_proj, b_proj, W_out, b_out, out):
         pc = keep.tile([P, B * NPB, BLK], U32, name="pc", align_bytes=64)
         psc = keep.tile([P, B * NPB, BLK], U8, name="psc", align_bytes=64)
         biasf = keep.tile([P, 8], F32, name="biasf")
+        xib = keep.tile([P, len(ECHUNKS), B * L], F32, name="xib")
 
         def x_transpose(g):
             xt = ps2.tile([P, T, P], BF16, name="xt", tag="s2")
@@ -213,6 +215,7 @@ def tile_srlbertold_pa_t_kernel(tc, seq_out, W_proj, b_proj, W_out, b_out, out):
             b, a, hh = u // (2 * NB), (u // 2) % NB, u % 2
             bank = ps1.tile([P, 2 * BLK], F32, name="bank", tag="s1")
             hs = slice(P * t, P * (t + 1))
+            as_bias = t in ECHUNKS and a <= 2 * hh and u >= 1
             for e in range(2):
                 c = 2 * hh + e
                 o = bank[:, BLK * e:BLK * (e + 1)]
@@ -225,11 +228,31 @@ def tile_srlbertold_pa_t_kernel(tc, seq_out, W_proj, b_proj, W_out, b_out, out):
                     first_c, first_s, second_c, second_s = xsc, xss, xfc, xfs
                 nc.tensor.matmul_mx(out=o, lhsT=wc[0][:, hs].bitcast(FP8X4), lhsT_scale=ws[0][:, hs],
                                     rhs=pc[:, i, :].bitcast(FP8X4), rhs_scale=psc[:, i, :], start=True, stop=False)
-                nc.tensor.matmul_mx(out=o, lhsT=wc[1][:, hs].bitcast(FP8X4), lhsT_scale=ws[1][:, hs],
-                                    rhs=first_c[:, sa].bitcast(FP8X4), rhs_scale=first_s[:, sa], start=False, stop=False)
+                if not as_bias:
+                    nc.tensor.matmul_mx(out=o, lhsT=wc[1][:, hs].bitcast(FP8X4), lhsT_scale=ws[1][:, hs],
+                                        rhs=first_c[:, sa].bitcast(FP8X4), rhs_scale=first_s[:, sa], start=False, stop=False)
                 nc.tensor.matmul_mx(out=o, lhsT=wc[2][:, hs].bitcast(FP8X4), lhsT_scale=ws[2][:, hs],
                                     rhs=second_c[:, scc].bitcast(FP8X4), rhs_scale=second_s[:, scc], start=False, stop=True)
-            nc.scalar.activation(out=pl[:, t, :], in_=bank[:], func=ACT.Tanh, bias=biasf[:, t:t + 1], scale=1.0)
+            if as_bias:
+                k = ECHUNKS.index(t)
+                for i in range(TB):
+                    tok = L * b + TB * a + i
+                    nc.scalar.activation(out=pl[:, t, :].rearrange("p (e i j) -> p e i j", e=2, i=TB)[:, :, i, :],
+                                         in_=bank[:].rearrange("p (e i j) -> p e i j", e=2, i=TB)[:, :, i, :],
+                                         func=ACT.Tanh, bias=xib[:, k, tok:tok + 1], scale=1.0)
+            else:
+                nc.scalar.activation(out=pl[:, t, :], in_=bank[:], func=ACT.Tanh, bias=biasf[:, t:t + 1], scale=1.0)
+
+        def first_term(g):
+            xi = ps1.tile([P, len(ECHUNKS), P], F32, name="xi", tag="s1")
+            for k in range(len(ECHUNKS)):
+                hs = slice(P * ECHUNKS[k], P * (ECHUNKS[k] + 1))
+                nc.tensor.matmul_mx(out=xi[:, k, :], lhsT=wc[1][:, hs].bitcast(FP8X4), lhsT_scale=ws[1][:, hs],
+                                    rhs=xc[:, P * g:P * (g + 1)].bitcast(FP8X4), rhs_scale=xs[:, P * g:P * (g + 1)],
+                                    start=True, stop=True)
+            for k in range(len(ECHUNKS)):
+                nc.scalar.activation(out=xib[:, k, P * g:P * (g + 1)], in_=xi[:, k, :], func=ACT.Identity,
+                                     bias=biasf[:, ECHUNKS[k]:ECHUNKS[k] + 1], scale=1.0)
 
         def stage2(u, qc, qs, ost):
             b, a, hh = u // (2 * NB), (u // 2) % NB, u % 2
@@ -266,6 +289,8 @@ def tile_srlbertold_pa_t_kernel(tc, seq_out, W_proj, b_proj, W_out, b_out, out):
                 if u2 % 2 == 0:
                     ostage[u2 // 2] = ring.tile([P, TB, L], F32, name="ost", tag="ost", bufs=3)
                 stage2(u2, codes[u2][0], codes[u2][1], ostage[u2 // 2])
+            if s == 1 or s == 2 * NB + 1:
+                first_term(s // (2 * NB))
             if s < UNITS:
                 planes[s] = ring.tile([P, T, 2 * BLK], BF16, name="pl", tag="pl", bufs=4)
                 for t in range(T):

@@ -14,8 +14,6 @@ FP8X4 = mybir.dt.float8_e4m3fn_x4
 ACT = mybir.ActivationFunctionType
 ALU = mybir.AluOpType
 
-MANUAL = True
-
 P = 128
 B = 4
 L = 64
@@ -27,7 +25,6 @@ BLK = TB * TB
 LAGD = 3
 PLEAD = 4
 ECHUNKS = (1, 3)
-UNITS = B * NB * 2
 
 
 def regroup(engine_copy, dst, src):
@@ -40,8 +37,7 @@ def regroup(engine_copy, dst, src):
 def tile_srlbertold_pa_t_kernel(tc, seq_out, W_proj, b_proj, W_out, b_out, out):
     nc = tc.nc
     with ExitStack() as ctx:
-        if MANUAL:
-            ctx.enter_context(tc.manual_schedule())
+        ctx.enter_context(tc.manual_schedule())
         keep = ctx.enter_context(tc.tile_pool(name="keep", bufs=1))
         ring = ctx.enter_context(tc.tile_pool(name="ring", bufs=3))
         ps1 = ctx.enter_context(tc.psum_pool(name="ps1", bufs=6))
@@ -178,32 +174,30 @@ def tile_srlbertold_pa_t_kernel(tc, seq_out, W_proj, b_proj, W_out, b_out, out):
             nc.vector.quantize_mx(out=wc[w][:, n0:n1].bitcast(FP8X4), scales=ws[w][:, n0:n1],
                                   in_=wg[w][:, n0:n1, :].rearrange("p n t -> p (n t)"))
 
+        PIECES = ((0, P), (P, 2 * P), (2 * P, H))
         x_transpose(0)
-        quant_x(0)
-        job0 = p_mul(0, 0, 0, 2)
-        w_regroup(nc.vector.tensor_copy, 0, 0, P)
-        w_regroup(nc.scalar.copy, 1, 0, P)
-        x40 = x_rep_a(0)
-        p_quant(job0)
-        w_quant(0, 0, P)
-        x_rep_b(0, x40)
-        w_regroup(nc.vector.tensor_copy, 2, 0, P)
-        x_rep_words(0)
-        w_quant(1, 0, P)
-        x_rep_scales(0)
-        w_quant(2, 0, P)
         bps = ps1.tile([P, P], BF16, name="bps", tag="s1")
         nc.tensor.transpose(bps[:], brows[:], ident[:])
+        for w in range(2):
+            for n0, n1 in PIECES:
+                w_regroup(nc.scalar.copy, w, n0, n1)
+        quant_x(0)
+        job0 = p_mul(0, 0, 0, 2)
+        x40 = x_rep_a(0)
+        p_quant(job0)
+        x_rep_b(0, x40)
+        x_rep_words(0)
+        x_rep_scales(0)
         nc.vector.tensor_copy(out=biasf[:], in_=bps[:, 0:8])
-        for n0, n1 in ((P, 2 * P), (2 * P, H)):
-            w_regroup(nc.scalar.copy, 1, n0, n1)
-            w_regroup(nc.vector.tensor_copy, 0, n0, n1)
-            w_regroup(nc.vector.tensor_copy, 2, n0, n1)
-            for w in range(3):
-                w_quant(w, n0, n1)
+        for n0, n1 in PIECES:
+            w_quant(0, n0, n1)
         job1 = p_mul(0, 0, 2, 4)
-        x_transpose(1)
+        for n0, n1 in PIECES:
+            w_regroup(nc.vector.tensor_copy, 2, n0, n1)
+            w_quant(1, n0, n1)
+            w_quant(2, n0, n1)
         p_quant(job1)
+        x_transpose(1)
         job2 = p_mul(0, 1, 1, 4)
         quant_x(1)
         p_quant(job2)
@@ -211,70 +205,84 @@ def tile_srlbertold_pa_t_kernel(tc, seq_out, W_proj, b_proj, W_out, b_out, out):
         regroup(nc.scalar.copy, wog[:], woraw[:])
         nc.vector.quantize_mx(out=woc[:].bitcast(FP8X4), scales=wos[:], in_=wog[:].rearrange("p n t -> p (n t)"))
 
-        def stage1(u, t, pl):
-            b, a, hh = u // (2 * NB), (u // 2) % NB, u % 2
-            bank = ps1.tile([P, 2 * BLK], F32, name="bank", tag="s1")
-            hs = slice(P * t, P * (t + 1))
-            as_bias = t in ECHUNKS and a <= 2 * hh and u >= 1
-            for e in range(2):
-                c = 2 * hh + e
-                o = bank[:, BLK * e:BLK * (e + 1)]
-                i = pidx[(b, min(a, c), max(a, c))]
-                sa = slice(BLK * (NB * b + a), BLK * (NB * b + a + 1))
-                scc = slice(BLK * (NB * b + c), BLK * (NB * b + c + 1))
-                if a <= c:
-                    first_c, first_s, second_c, second_s = xfc, xfs, xsc, xss
+        units = []
+        for b in range(B):
+            for a in range(NB):
+                units.append((b, a, 0, 2))
+                if (b, a) == (B - 1, NB - 1):
+                    units.append((b, a, 2, 1))
+                    units.append((b, a, 3, 1))
                 else:
-                    first_c, first_s, second_c, second_s = xsc, xss, xfc, xfs
-                nc.tensor.matmul_mx(out=o, lhsT=wc[0][:, hs].bitcast(FP8X4), lhsT_scale=ws[0][:, hs],
-                                    rhs=pc[:, i, :].bitcast(FP8X4), rhs_scale=psc[:, i, :], start=True, stop=False)
-                if not as_bias:
-                    nc.tensor.matmul_mx(out=o, lhsT=wc[1][:, hs].bitcast(FP8X4), lhsT_scale=ws[1][:, hs],
-                                        rhs=first_c[:, sa].bitcast(FP8X4), rhs_scale=first_s[:, sa], start=False, stop=False)
-                nc.tensor.matmul_mx(out=o, lhsT=wc[2][:, hs].bitcast(FP8X4), lhsT_scale=ws[2][:, hs],
-                                    rhs=second_c[:, scc].bitcast(FP8X4), rhs_scale=second_s[:, scc], start=False, stop=True)
-            if as_bias:
+                    units.append((b, a, 2, 2))
+        NU = len(units)
+
+        def mx(o, w, t, rc, rs, start, stop):
+            hs = slice(P * t, P * (t + 1))
+            nc.tensor.matmul_mx(out=o, lhsT=wc[w][:, hs].bitcast(FP8X4), lhsT_scale=ws[w][:, hs],
+                                rhs=rc.bitcast(FP8X4), rhs_scale=rs, start=start, stop=stop)
+
+        def stage1(u, t, pl):
+            b, a, c0, n = units[u]
+            bank = ps1.tile([P, n * BLK], F32, name="bank", tag="s1")
+            if t in ECHUNKS and a <= c0 and n == 2 and u >= 1:
+                i0 = pidx[(b, a, c0)]
+                sc2 = slice(BLK * (NB * b + c0), BLK * (NB * b + c0 + 2))
+                mx(bank[:], 0, t, pc[:, i0:i0 + 2, :].rearrange("p n w -> p (n w)"),
+                   psc[:, i0:i0 + 2, :].rearrange("p n w -> p (n w)"), True, False)
+                mx(bank[:], 2, t, xsc[:, sc2], xss[:, sc2], False, True)
                 k = ECHUNKS.index(t)
                 for i in range(TB):
                     tok = L * b + TB * a + i
                     nc.scalar.activation(out=pl[:, t, :].rearrange("p (e i j) -> p e i j", e=2, i=TB)[:, :, i, :],
                                          in_=bank[:].rearrange("p (e i j) -> p e i j", e=2, i=TB)[:, :, i, :],
                                          func=ACT.Tanh, bias=xib[:, k, tok:tok + 1], scale=1.0)
-            else:
-                nc.scalar.activation(out=pl[:, t, :], in_=bank[:], func=ACT.Tanh, bias=biasf[:, t:t + 1], scale=1.0)
+                return
+            for e in range(n):
+                c = c0 + e
+                o = bank[:, BLK * e:BLK * (e + 1)]
+                i = pidx[(b, min(a, c), max(a, c))]
+                sa = slice(BLK * (NB * b + a), BLK * (NB * b + a + 1))
+                scc = slice(BLK * (NB * b + c), BLK * (NB * b + c + 1))
+                mx(o, 0, t, pc[:, i, :], psc[:, i, :], True, False)
+                if a <= c:
+                    mx(o, 1, t, xfc[:, sa], xfs[:, sa], False, False)
+                    mx(o, 2, t, xsc[:, scc], xss[:, scc], False, True)
+                else:
+                    mx(o, 1, t, xsc[:, sa], xss[:, sa], False, False)
+                    mx(o, 2, t, xfc[:, scc], xfs[:, scc], False, True)
+            nc.scalar.activation(out=pl[:, t, :], in_=bank[:], func=ACT.Tanh, bias=biasf[:, t:t + 1], scale=1.0)
 
         def first_term(g):
             xi = ps1.tile([P, len(ECHUNKS), P], F32, name="xi", tag="s1")
             for k in range(len(ECHUNKS)):
-                hs = slice(P * ECHUNKS[k], P * (ECHUNKS[k] + 1))
-                nc.tensor.matmul_mx(out=xi[:, k, :], lhsT=wc[1][:, hs].bitcast(FP8X4), lhsT_scale=ws[1][:, hs],
-                                    rhs=xc[:, P * g:P * (g + 1)].bitcast(FP8X4), rhs_scale=xs[:, P * g:P * (g + 1)],
-                                    start=True, stop=True)
+                mx(xi[:, k, :], 1, ECHUNKS[k], xc[:, P * g:P * (g + 1)], xs[:, P * g:P * (g + 1)], True, True)
             for k in range(len(ECHUNKS)):
                 nc.scalar.activation(out=xib[:, k, P * g:P * (g + 1)], in_=xi[:, k, :], func=ACT.Identity,
                                      bias=biasf[:, ECHUNKS[k]:ECHUNKS[k] + 1], scale=1.0)
 
         def stage2(u, qc, qs, ost):
-            b, a, hh = u // (2 * NB), (u // 2) % NB, u % 2
-            bank2 = ps2.tile([P, 2 * BLK], F32, name="bank2", tag="s2")
+            b, a, c0, n = units[u]
+            bank2 = ps2.tile([P, n * BLK], F32, name="bank2", tag="s2")
             nc.tensor.matmul_mx(out=bank2[:], lhsT=woc[:].bitcast(FP8X4), lhsT_scale=wos[:],
                                 rhs=qc[:].bitcast(FP8X4), rhs_scale=qs[:], start=True, stop=True)
-            c = 2 * hh
-            if a <= c or a > c + 1:
-                if a <= c:
+            if n == 2 and (a <= c0 or a > c0 + 1):
+                if a <= c0:
                     view = bank2[:].rearrange("p (e f s) -> p f e s", e=2, f=TB)
                 else:
                     view = bank2[:].rearrange("p (e s f) -> p f e s", e=2, s=TB)
-                nc.scalar.activation(out=ost[:, :, TB * c:TB * (c + 2)].rearrange("p f (e s) -> p f e s", e=2),
+                nc.scalar.activation(out=ost[:, :, TB * c0:TB * (c0 + 2)].rearrange("p f (e s) -> p f e s", e=2),
                                      in_=view, func=ACT.Identity, bias=biasf[:, 4:5], scale=1.0)
             else:
-                nc.scalar.activation(out=ost[:, :, TB * c:TB * (c + 1)],
-                                     in_=bank2[:, 0:BLK].rearrange("p (s f) -> p f s", s=TB),
-                                     func=ACT.Identity, bias=biasf[:, 4:5], scale=1.0)
-                nc.scalar.activation(out=ost[:, :, TB * (c + 1):TB * (c + 2)],
-                                     in_=bank2[:, BLK:2 * BLK].rearrange("p (f s) -> p f s", f=TB),
-                                     func=ACT.Identity, bias=biasf[:, 4:5], scale=1.0)
-            if hh == 1:
+                for e in range(n):
+                    c = c0 + e
+                    blk = bank2[:, BLK * e:BLK * (e + 1)]
+                    if a <= c:
+                        view = blk.rearrange("p (f s) -> p f s", f=TB)
+                    else:
+                        view = blk.rearrange("p (s f) -> p f s", s=TB)
+                    nc.scalar.activation(out=ost[:, :, TB * c:TB * (c + 1)], in_=view, func=ACT.Identity,
+                                         bias=biasf[:, 4:5], scale=1.0)
+            if c0 + n == NB:
                 nc.sync.dma_start(out=out[b, :, TB * a:TB * (a + 1), :].rearrange("k f s -> k (f s)"),
                                   in_=ost[:].rearrange("p f s -> p (f s)"))
 
@@ -283,33 +291,35 @@ def tile_srlbertold_pa_t_kernel(tc, seq_out, W_proj, b_proj, W_out, b_out, out):
         ostage = {}
         pending = []
         x4n = x40
-        for s in range(UNITS + LAGD):
+        for s in range(NU + LAGD):
             u2 = s - LAGD
             if u2 >= 0:
-                if u2 % 2 == 0:
-                    ostage[u2 // 2] = ring.tile([P, TB, L], F32, name="ost", tag="ost", bufs=3)
-                stage2(u2, codes[u2][0], codes[u2][1], ostage[u2 // 2])
+                row = units[u2][0:2]
+                if units[u2][2] == 0:
+                    ostage[row] = ring.tile([P, TB, L], F32, name="ost", tag="ost", bufs=3)
+                stage2(u2, codes[u2][0], codes[u2][1], ostage[row])
             if s == 1 or s == 2 * NB + 1:
                 first_term(s // (2 * NB))
-            if s < UNITS:
-                planes[s] = ring.tile([P, T, 2 * BLK], BF16, name="pl", tag="pl", bufs=4)
+            if s < NU:
+                planes[s] = ring.tile([P, T, units[s][3] * BLK], BF16, name="pl", tag="pl", bufs=4)
                 for t in range(T):
                     stage1(s, t, planes[s])
             u1 = s - 1
-            if 0 <= u1 < UNITS:
-                g2 = ring.tile([P, 2 * BLK, T], BF16, name="g2", tag="g2", align_bytes=64, bufs=3)
+            if 0 <= u1 < NU:
+                n1 = units[u1][3] * BLK
+                g2 = ring.tile([P, n1, T], BF16, name="g2", tag="g2", align_bytes=64, bufs=3)
                 regroup(nc.vector.tensor_copy, g2[:], planes[u1][:])
             for job in pending:
                 p_quant(job)
             pending = []
-            if 0 <= u1 < UNITS:
-                qc = ring.tile([P, 2 * BLK], U32, name="qc", tag="qc", align_bytes=64, bufs=LAGD + 2)
-                qs = ring.tile([P, 2 * BLK], U8, name="qs", tag="qs", align_bytes=64, bufs=LAGD + 2)
+            if 0 <= u1 < NU:
+                qc = ring.tile([P, n1], U32, name="qc", tag="qc", align_bytes=64, bufs=LAGD + 2)
+                qs = ring.tile([P, n1], U8, name="qs", tag="qs", align_bytes=64, bufs=LAGD + 2)
                 nc.vector.quantize_mx(out=qc[:].bitcast(FP8X4), scales=qs[:], in_=g2[:].rearrange("p n t -> p (n t)"))
                 codes[u1] = (qc, qs)
             r = s + PLEAD
-            if r % 2 == 0 and r < UNITS:
-                pending.append(p_mul(r // (2 * NB), (r // 2) % NB, (r // 2) % NB, NB))
+            if r < NU and units[r][2] == 0:
+                pending.append(p_mul(units[r][0], units[r][1], units[r][1], NB))
             nb = s // (2 * NB) + 1
             if nb < B:
                 if s % (2 * NB) == 1:

@@ -24,7 +24,7 @@ NB = L // TB
 BLK = TB * TB
 LAGD = 3
 PLEAD = 4
-ECHUNKS = (1, 3)
+ECHUNKS = (1, 2, 3)
 
 
 def regroup(engine_copy, dst, src):

@@ -22,7 +22,7 @@ T = 4
 TB = 16
 NB = L // TB
 BLK = TB * TB
-LAGD = 3
+LAGD = 4
 PLEAD = 4
 ECHUNKS = (1, 2, 3)
 
@@ -191,13 +191,12 @@ def tile_srlbertold_pa_t_kernel(tc, seq_out, W_proj, b_proj, W_out, b_out, out):
         nc.vector.tensor_copy(out=biasf[:], in_=bps[:, 0:8])
         for n0, n1 in PIECES:
             w_quant(0, n0, n1)
-        job1 = p_mul(0, 0, 2, 4)
-        for n0, n1 in PIECES:
             w_regroup(nc.vector.tensor_copy, 2, n0, n1)
             w_quant(1, n0, n1)
             w_quant(2, n0, n1)
-        p_quant(job1)
+        job1 = p_mul(0, 0, 2, 4)
         x_transpose(1)
+        p_quant(job1)
         job2 = p_mul(0, 1, 1, 4)
         quant_x(1)
         p_quant(job2)
@@ -301,7 +300,7 @@ def tile_srlbertold_pa_t_kernel(tc, seq_out, W_proj, b_proj, W_out, b_out, out):
             if s == 1 or s == 2 * NB + 1:
                 first_term(s // (2 * NB))
             if s < NU:
-                planes[s] = ring.tile([P, T, units[s][3] * BLK], BF16, name="pl", tag="pl", bufs=4)
+                planes[s] = ring.tile([P, T, units[s][3] * BLK], BF16, name="pl", tag="pl", bufs=LAGD + 1)
                 for t in range(T):
                     stage1(s, t, planes[s])
             u1 = s - 1

@@ -269,8 +269,11 @@ def tile_srlbertold_pa_t_kernel(tc, seq_out, W_proj, b_proj, W_out, b_out, out):
                     view = bank2[:].rearrange("p (e f s) -> p f e s", e=2, f=TB)
                 else:
                     view = bank2[:].rearrange("p (e s f) -> p f e s", e=2, s=TB)
-                nc.scalar.activation(out=ost[:, :, TB * c0:TB * (c0 + 2)].rearrange("p f (e s) -> p f e s", e=2),
-                                     in_=view, func=ACT.Identity, bias=biasf[:, 4:5], scale=1.0)
+                dst = ost[:, :, TB * c0:TB * (c0 + 2)].rearrange("p f (e s) -> p f e s", e=2)
+                if u % 4 == 0:
+                    nc.vector.tensor_scalar(out=dst, in0=view, scalar1=biasf[:, 4:5], scalar2=None, op0=ALU.add)
+                else:
+                    nc.scalar.activation(out=dst, in_=view, func=ACT.Identity, bias=biasf[:, 4:5], scale=1.0)
             else:
                 for e in range(n):
                     c = c0 + e

@@ -22,7 +22,7 @@ T = 4
 TB = 16
 NB = L // TB
 BLK = TB * TB
-LAGD = 4
+LAGD = 5
 PLEAD = 4
 ECHUNKS = (1, 2, 3)
 
@@ -44,17 +44,20 @@ def tile_srlbertold_pa_t_kernel(tc, seq_out, W_proj, b_proj, W_out, b_out, out):
         ps2 = ctx.enter_context(tc.psum_pool(name="ps2", bufs=2))
 
         x_sb = keep.tile([P, 2, H], BF16, name="x_sb")
-        nc.sync.dma_start(out=x_sb[:], in_=seq_out.rearrange("b l h -> (b l) h").rearrange("(g p) h -> p g h", p=P))
+        x_rows = seq_out.rearrange("b l h -> (b l) h").rearrange("(g p) h -> p g h", p=P)
+        nc.sync.dma_start(out=x_sb[:, 0, :], in_=x_rows[:, 0, :])
         brows = keep.tile([P, P], BF16, name="brows")
         nc.vector.memset(brows[:], 0.0)
+        nc.sync.dma_start(out=brows[0:4, :], in_=b_proj.rearrange("(t p) -> t p", p=P))
+        nc.sync.dma_start(out=brows[4:5, :], in_=b_out.rearrange("(o k) -> o k", o=1))
         wraw = []
         for w in range(3):
             wr = keep.tile([P, T, H], BF16, name="wraw%d" % w)
-            nc.sync.dma_start(out=wr[:], in_=W_proj[H * w:H * (w + 1), :].rearrange("(t p) n -> p t n", p=P))
             wraw.append(wr)
-            if w == 0:
-                nc.sync.dma_start(out=brows[0:4, :], in_=b_proj.rearrange("(t p) -> t p", p=P))
-                nc.sync.dma_start(out=brows[4:5, :], in_=b_out.rearrange("(o k) -> o k", o=1))
+        for n0, n1 in ((0, P), (P, H)):
+            for w in range(3):
+                nc.sync.dma_start(out=wraw[w][:, :, n0:n1], in_=W_proj[H * w:H * (w + 1), n0:n1].rearrange("(t p) n -> p t n", p=P))
+        nc.sync.dma_start(out=x_sb[:, 1, :], in_=x_rows[:, 1, :])
         woraw = keep.tile([P, T, P], BF16, name="woraw")
         nc.sync.dma_start(out=woraw[:], in_=W_out.rearrange("(t p) n -> p t n", p=P))
 
@@ -68,14 +71,12 @@ def tile_srlbertold_pa_t_kernel(tc, seq_out, W_proj, b_proj, W_out, b_out, out):
         xg = keep.tile([P, B * L, T], BF16, name="xg", align_bytes=64)
         xc = keep.tile([P, B * L], U32, name="xc", align_bytes=64)
         xs = keep.tile([P, B * L], U8, name="xs", align_bytes=64)
-        x4c = keep.tile([P, B * L * 4], U32, name="x4c", align_bytes=64)
         x4s = keep.tile([P, B * L * 4], U8, name="x4s", align_bytes=64)
         xfc = keep.tile([P, B * L * TB], U32, name="xfc", align_bytes=64)
         xfs = keep.tile([P, B * L * TB], U8, name="xfs", align_bytes=64)
         xsc = keep.tile([P, B * L * TB], U32, name="xsc", align_bytes=64)
         xss = keep.tile([P, B * L * TB], U8, name="xss", align_bytes=64)
         nc.vector.memset(xs[:].bitcast(I32), 0)
-        nc.vector.memset(x4s[:].bitcast(I32), 0)
         wg = [keep.tile([P, H, T], BF16, name="wg%d" % w, align_bytes=64) for w in range(3)]
         wc = [keep.tile([P, H], U32, name="wc%d" % w, align_bytes=64) for w in range(3)]
         ws = [keep.tile([P, H], U8, name="ws%d" % w, align_bytes=64) for w in range(3)]
@@ -100,17 +101,9 @@ def tile_srlbertold_pa_t_kernel(tc, seq_out, W_proj, b_proj, W_out, b_out, out):
                 in_=xg[:, P * g:P * (g + 1), :].rearrange("p r t -> p (r t)"),
             )
 
-        def x_rep_a(b):
-            x4 = ring.tile([P, L, 4, T], BF16, name="x4", tag="x4", align_bytes=64, bufs=2)
-            nc.vector.tensor_copy(out=x4[:], in_=xg[:, L * b:L * (b + 1), :].unsqueeze(2).to_broadcast([P, L, 4, T]))
-            return x4
-
-        def x_rep_b(b, x4):
-            nc.vector.quantize_mx(
-                out=x4c[:, 4 * L * b:4 * L * (b + 1)].bitcast(FP8X4),
-                scales=x4s[:, 4 * L * b:4 * L * (b + 1)],
-                in_=x4[:].rearrange("p r q t -> p (r q t)"),
-            )
+        def x_rep_four(b):
+            for q in range(4):
+                nc.vector.tensor_copy(out=x4s[:, 4 * L * b + q:4 * L * (b + 1):4], in_=xs[:, L * b:L * (b + 1)])
 
         NX = L * TB
 
@@ -178,14 +171,13 @@ def tile_srlbertold_pa_t_kernel(tc, seq_out, W_proj, b_proj, W_out, b_out, out):
         x_transpose(0)
         bps = ps1.tile([P, P], BF16, name="bps", tag="s1")
         nc.tensor.transpose(bps[:], brows[:], ident[:])
-        for w in range(2):
-            for n0, n1 in PIECES:
+        for n0, n1 in PIECES:
+            for w in range(2):
                 w_regroup(nc.scalar.copy, w, n0, n1)
         quant_x(0)
         job0 = p_mul(0, 0, 0, 2)
-        x40 = x_rep_a(0)
+        x_rep_four(0)
         p_quant(job0)
-        x_rep_b(0, x40)
         x_rep_words(0)
         x_rep_scales(0)
         nc.vector.tensor_copy(out=biasf[:], in_=bps[:, 0:8])
@@ -236,7 +228,16 @@ def tile_srlbertold_pa_t_kernel(tc, seq_out, W_proj, b_proj, W_out, b_out, out):
                                          in_=bank[:].rearrange("p (e i j) -> p e i j", e=2, i=TB)[:, :, i, :],
                                          func=ACT.Tanh, bias=xib[:, k, tok:tok + 1], scale=1.0)
                 return
-            for e in range(n):
+            if n == 2 and a <= c0:
+                i0 = pidx[(b, a, c0)]
+                sa = slice(BLK * (NB * b + a), BLK * (NB * b + a + 1))
+                sc2 = slice(BLK * (NB * b + c0), BLK * (NB * b + c0 + 2))
+                mx(bank[:], 0, t, pc[:, i0:i0 + 2, :].rearrange("p n w -> p (n w)"),
+                   psc[:, i0:i0 + 2, :].rearrange("p n w -> p (n w)"), True, False)
+                mx(bank[:, 0:BLK], 1, t, xfc[:, sa], xfs[:, sa], False, False)
+                mx(bank[:, BLK:], 1, t, xfc[:, sa], xfs[:, sa], False, False)
+                mx(bank[:], 2, t, xsc[:, sc2], xss[:, sc2], False, True)
+            for e in range(n if n == 1 or a > c0 else 0):
                 c = c0 + e
                 o = bank[:, BLK * e:BLK * (e + 1)]
                 i = pidx[(b, min(a, c), max(a, c))]
@@ -292,7 +293,6 @@ def tile_srlbertold_pa_t_kernel(tc, seq_out, W_proj, b_proj, W_out, b_out, out):
         codes = {}
         ostage = {}
         pending = []
-        x4n = x40
         for s in range(NU + LAGD):
             u2 = s - LAGD
             if u2 >= 0:
@@ -314,20 +314,19 @@ def tile_srlbertold_pa_t_kernel(tc, seq_out, W_proj, b_proj, W_out, b_out, out):
             for job in pending:
                 p_quant(job)
             pending = []
+            r = s + PLEAD
+            if r < NU and units[r][2] == 0:
+                pending.append(p_mul(units[r][0], units[r][1], units[r][1], NB))
             if 0 <= u1 < NU:
                 qc = ring.tile([P, n1], U32, name="qc", tag="qc", align_bytes=64, bufs=LAGD + 2)
                 qs = ring.tile([P, n1], U8, name="qs", tag="qs", align_bytes=64, bufs=LAGD + 2)
                 nc.vector.quantize_mx(out=qc[:].bitcast(FP8X4), scales=qs[:], in_=g2[:].rearrange("p n t -> p (n t)"))
                 codes[u1] = (qc, qs)
-            r = s + PLEAD
-            if r < NU and units[r][2] == 0:
-                pending.append(p_mul(units[r][0], units[r][1], units[r][1], NB))
             nb = s // (2 * NB) + 1
             if nb < B:
                 if s % (2 * NB) == 1:
-                    x4n = x_rep_a(nb)
                     x_rep_words(nb)
                 if s % (2 * NB) == 3:
-                    x_rep_b(nb, x4n)
+                    x_rep_four(nb)
                 if s % (2 * NB) == 5:
                     x_rep_scales(nb)

@@ -29,8 +29,8 @@ ECHUNKS = (1, 2, 3)
 
 def regroup(engine_copy, dst, src):
     engine_copy(
-        out=dst.rearrange("p (c i) t -> p c t i", i=4),
-        in_=src.rearrange("p t (c i) -> p c t i", i=4),
+        out=dst.rearrange("p (c i) t -> p c t i", i=8),
+        in_=src.rearrange("p t (c i) -> p c t i", i=8),
     )
 
 
@@ -92,7 +92,10 @@ def tile_srlbertold_pa_t_kernel(tc, seq_out, W_proj, b_proj, W_out, b_out, out):
             xt = ps2.tile([P, T, P], BF16, name="xt", tag="s2")
             for t in range(T):
                 nc.tensor.transpose(xt[:, t, :], x_sb[:, g, P * t:P * (t + 1)], ident[:])
-            nc.vector.tensor_copy(out=xg[:, P * g:P * (g + 1), :], in_=xt[:].rearrange("p t r -> p r t"))
+            return xt
+
+        def x_copy(g, xt, b0, b1):
+            nc.vector.tensor_copy(out=xg[:, L * b0:L * b1, :], in_=xt[:, :, L * b0 - P * g:L * b1 - P * g].rearrange("p t r -> p r t"))
 
         def quant_x(g):
             nc.vector.quantize_mx(
@@ -107,25 +110,27 @@ def tile_srlbertold_pa_t_kernel(tc, seq_out, W_proj, b_proj, W_out, b_out, out):
 
         NX = L * TB
 
-        def x_rep_words(b):
+        def x_outer(b, c0=0, c1=NB):
+            n0, n1 = NX * b + BLK * c0, NX * b + BLK * c1
+            t0, t1 = L * b + TB * c0, L * b + TB * c1
             nc.vector.tensor_copy(
-                out=xfc[:, NX * b:NX * (b + 1)].bitcast(I32).rearrange("p (r q) -> p r q", q=TB),
-                in_=xc[:, L * b:L * (b + 1)].bitcast(I32).unsqueeze(2).to_broadcast([P, L, TB]),
+                out=xfc[:, n0:n1].bitcast(I32).rearrange("p (r q) -> p r q", q=TB),
+                in_=xc[:, t0:t1].bitcast(I32).unsqueeze(2).to_broadcast([P, t1 - t0, TB]),
             )
             nc.vector.tensor_copy(
-                out=xsc[:, NX * b:NX * (b + 1)].bitcast(I32).rearrange("p (c q j) -> p c q j", q=TB, j=TB),
-                in_=xc[:, L * b:L * (b + 1)].bitcast(I32).rearrange("p (c j) -> p c j", j=TB).unsqueeze(2).to_broadcast([P, NB, TB, TB]),
+                out=xfs[:, n0:n1].bitcast(I32).rearrange("p (r q) -> p r q", q=TB // 4),
+                in_=x4s[:, 4 * t0:4 * t1].bitcast(I32).unsqueeze(2).to_broadcast([P, t1 - t0, TB // 4]),
             )
 
-        def x_rep_scales(b):
-            nc.vector.tensor_copy(
-                out=xfs[:, NX * b:NX * (b + 1)].bitcast(I32).rearrange("p (r q) -> p r q", q=TB // 4),
-                in_=x4s[:, 4 * L * b:4 * L * (b + 1)].bitcast(I32).unsqueeze(2).to_broadcast([P, L, TB // 4]),
-            )
-            nc.vector.tensor_copy(
-                out=xss[:, NX * b:NX * (b + 1)].bitcast(I32).rearrange("p (c q j) -> p c q j", q=TB, j=TB // 4),
-                in_=xs[:, L * b:L * (b + 1)].bitcast(I32).rearrange("p (c j) -> p c j", j=TB // 4).unsqueeze(2).to_broadcast([P, NB, TB, TB // 4]),
-            )
+        def x_inner(b, c0=0, c1=NB):
+            n0, n1 = NX * b + BLK * c0, NX * b + BLK * c1
+            t0, t1 = L * b + TB * c0, L * b + TB * c1
+            for dst, src_x in ((xsc, xc), (xss, xs)):
+                src = src_x[:, t0:t1].bitcast(I32).rearrange("p (c j) -> p c j", c=c1 - c0)
+                nc.vector.tensor_copy(
+                    out=dst[:, n0:n1].bitcast(I32).rearrange("p (c q j) -> p c q j", c=c1 - c0, q=TB),
+                    in_=src.unsqueeze(2).to_broadcast([P, c1 - c0, TB, src.shape[2]]),
+                )
 
         pidx = {}
         for b in range(B):
@@ -167,34 +172,42 @@ def tile_srlbertold_pa_t_kernel(tc, seq_out, W_proj, b_proj, W_out, b_out, out):
             nc.vector.quantize_mx(out=wc[w][:, n0:n1].bitcast(FP8X4), scales=ws[w][:, n0:n1],
                                   in_=wg[w][:, n0:n1, :].rearrange("p n t -> p (n t)"))
 
-        PIECES = ((0, P), (P, 2 * P), (2 * P, H))
-        x_transpose(0)
+        PIECES = tuple((P * t, P * (t + 1)) for t in range(T))
+        xt0 = x_transpose(0)
         bps = ps1.tile([P, P], BF16, name="bps", tag="s1")
         nc.tensor.transpose(bps[:], brows[:], ident[:])
-        for n0, n1 in PIECES:
+        for w in range(3):
+            w_regroup(nc.scalar.copy, w, *PIECES[0])
+        for piece in PIECES[1:]:
             for w in range(2):
-                w_regroup(nc.scalar.copy, w, n0, n1)
-        quant_x(0)
+                w_regroup(nc.scalar.copy, w, *piece)
+        x_copy(0, xt0, 0, 1)
         job0 = p_mul(0, 0, 0, 2)
-        x_rep_four(0)
+        x_copy(0, xt0, 1, 2)
         p_quant(job0)
-        x_rep_words(0)
-        x_rep_scales(0)
+        w_quant(0, *PIECES[0])
+        quant_x(0)
+        w_quant(1, *PIECES[0])
+        x_rep_four(0)
+        w_quant(2, *PIECES[0])
+        x_outer(0, 0, 1)
+        x_inner(0, 0, 2)
         nc.vector.tensor_copy(out=biasf[:], in_=bps[:, 0:8])
-        for n0, n1 in PIECES:
-            w_quant(0, n0, n1)
+        w_regroup(nc.vector.tensor_copy, 2, *PIECES[1])
+        for w in range(3):
+            w_quant(w, *PIECES[1])
+        x_inner(0, 2, 4)
+        job1 = p_mul(0, 0, 2, 4)
+        for n0, n1 in PIECES[2:]:
             w_regroup(nc.vector.tensor_copy, 2, n0, n1)
+            w_quant(0, n0, n1)
             w_quant(1, n0, n1)
             w_quant(2, n0, n1)
-        job1 = p_mul(0, 0, 2, 4)
-        x_transpose(1)
         p_quant(job1)
+        x_outer(0, 1, 4)
         job2 = p_mul(0, 1, 1, 4)
-        quant_x(1)
-        p_quant(job2)
         wog = keep.tile([P, P, T], BF16, name="wog", align_bytes=64)
-        regroup(nc.scalar.copy, wog[:], woraw[:])
-        nc.vector.quantize_mx(out=woc[:].bitcast(FP8X4), scales=wos[:], in_=wog[:].rearrange("p n t -> p (n t)"))
+        p_quant(job2)
 
         units = []
         for b in range(B):
@@ -306,6 +319,8 @@ def tile_srlbertold_pa_t_kernel(tc, seq_out, W_proj, b_proj, W_out, b_out, out):
                 planes[s] = ring.tile([P, T, units[s][3] * BLK], BF16, name="pl", tag="pl", bufs=LAGD + 1)
                 for t in range(T):
                     stage1(s, t, planes[s])
+            if s == 1:
+                regroup(nc.scalar.copy, wog[:], woraw[:])
             u1 = s - 1
             if 0 <= u1 < NU:
                 n1 = units[u1][3] * BLK
@@ -322,11 +337,16 @@ def tile_srlbertold_pa_t_kernel(tc, seq_out, W_proj, b_proj, W_out, b_out, out):
                 qs = ring.tile([P, n1], U8, name="qs", tag="qs", align_bytes=64, bufs=LAGD + 2)
                 nc.vector.quantize_mx(out=qc[:].bitcast(FP8X4), scales=qs[:], in_=g2[:].rearrange("p n t -> p (n t)"))
                 codes[u1] = (qc, qs)
+            if s == 2:
+                nc.vector.quantize_mx(out=woc[:].bitcast(FP8X4), scales=wos[:], in_=wog[:].rearrange("p n t -> p (n t)"))
+                x_copy(1, x_transpose(1), 2, 4)
+            if s == 4:
+                quant_x(1)
             nb = s // (2 * NB) + 1
             if nb < B:
                 if s % (2 * NB) == 1:
-                    x_rep_words(nb)
+                    x_inner(nb)
                 if s % (2 * NB) == 3:
                     x_rep_four(nb)
                 if s % (2 * NB) == 5:
-                    x_rep_scales(nb)
+                    x_outer(nb)

@@ -22,9 +22,11 @@ T = 4
 TB = 16
 NB = L // TB
 BLK = TB * TB
-LAGD = 5
-PLEAD = 4
+HT = TB // 2
+HB = BLK // 2
 ECHUNKS = (1, 2, 3)
+EMPTIED_BY_VECTOR = ("row0a",)
+LAGD = 5
 
 
 def regroup(engine_copy, dst, src):
@@ -39,9 +41,9 @@ def tile_srlbertold_pa_t_kernel(tc, seq_out, W_proj, b_proj, W_out, b_out, out):
     with ExitStack() as ctx:
         ctx.enter_context(tc.manual_schedule())
         keep = ctx.enter_context(tc.tile_pool(name="keep", bufs=1))
-        ring = ctx.enter_context(tc.tile_pool(name="ring", bufs=3))
-        ps1 = ctx.enter_context(tc.psum_pool(name="ps1", bufs=6))
-        ps2 = ctx.enter_context(tc.psum_pool(name="ps2", bufs=2))
+        ring = ctx.enter_context(tc.tile_pool(name="ring", bufs=2))
+        ps1 = ctx.enter_context(tc.psum_pool(name="ps1", bufs=5))
+        ps2 = ctx.enter_context(tc.psum_pool(name="ps2", bufs=3))
 
         x_sb = keep.tile([P, 2, H], BF16, name="x_sb")
         x_rows = seq_out.rearrange("b l h -> (b l) h").rearrange("(g p) h -> p g h", p=P)
@@ -50,12 +52,11 @@ def tile_srlbertold_pa_t_kernel(tc, seq_out, W_proj, b_proj, W_out, b_out, out):
         nc.vector.memset(brows[:], 0.0)
         nc.sync.dma_start(out=brows[0:4, :], in_=b_proj.rearrange("(t p) -> t p", p=P))
         nc.sync.dma_start(out=brows[4:5, :], in_=b_out.rearrange("(o k) -> o k", o=1))
-        wraw = []
-        for w in range(3):
-            wr = keep.tile([P, T, H], BF16, name="wraw%d" % w)
-            wraw.append(wr)
+        wraw = {}
+        for w in (0, 2, 1):
+            wraw[w] = keep.tile([P, T, H], BF16, name="wraw%d" % w)
         for n0, n1 in ((0, P), (P, H)):
-            for w in range(3):
+            for w in (0, 2, 1):
                 nc.sync.dma_start(out=wraw[w][:, :, n0:n1], in_=W_proj[H * w:H * (w + 1), n0:n1].rearrange("(t p) n -> p t n", p=P))
         nc.sync.dma_start(out=x_sb[:, 1, :], in_=x_rows[:, 1, :])
         woraw = keep.tile([P, T, P], BF16, name="woraw")
@@ -71,22 +72,15 @@ def tile_srlbertold_pa_t_kernel(tc, seq_out, W_proj, b_proj, W_out, b_out, out):
         xg = keep.tile([P, B * L, T], BF16, name="xg", align_bytes=64)
         xc = keep.tile([P, B * L], U32, name="xc", align_bytes=64)
         xs = keep.tile([P, B * L], U8, name="xs", align_bytes=64)
-        x4s = keep.tile([P, B * L * 4], U8, name="x4s", align_bytes=64)
-        xfc = keep.tile([P, B * L * TB], U32, name="xfc", align_bytes=64)
-        xfs = keep.tile([P, B * L * TB], U8, name="xfs", align_bytes=64)
-        xsc = keep.tile([P, B * L * TB], U32, name="xsc", align_bytes=64)
-        xss = keep.tile([P, B * L * TB], U8, name="xss", align_bytes=64)
         nc.vector.memset(xs[:].bitcast(I32), 0)
+        x4s = keep.tile([P, B * L * 4], U8, name="x4s", align_bytes=64)
         wg = [keep.tile([P, H, T], BF16, name="wg%d" % w, align_bytes=64) for w in range(3)]
         wc = [keep.tile([P, H], U32, name="wc%d" % w, align_bytes=64) for w in range(3)]
         ws = [keep.tile([P, H], U8, name="ws%d" % w, align_bytes=64) for w in range(3)]
         woc = keep.tile([P, P], U32, name="woc", align_bytes=64)
         wos = keep.tile([P, P], U8, name="wos", align_bytes=64)
-        NPB = NB * (NB + 1) // 2
-        pc = keep.tile([P, B * NPB, BLK], U32, name="pc", align_bytes=64)
-        psc = keep.tile([P, B * NPB, BLK], U8, name="psc", align_bytes=64)
         biasf = keep.tile([P, 8], F32, name="biasf")
-        xib = keep.tile([P, len(ECHUNKS), B * L], F32, name="xib")
+        xbias = keep.tile([P, T, B * L], F32, name="xbias")
 
         def x_transpose(g):
             xt = ps2.tile([P, T, P], BF16, name="xt", tag="s2")
@@ -104,66 +98,104 @@ def tile_srlbertold_pa_t_kernel(tc, seq_out, W_proj, b_proj, W_out, b_out, out):
                 in_=xg[:, P * g:P * (g + 1), :].rearrange("p r t -> p (r t)"),
             )
 
-        def x_rep_four(b):
+        NCOL = 2 * BLK
+        IN1 = NCOL - BLK
+        xin = {}
+        xout = {}
+
+        def spread(dst, src, q, by_dma):
+            n = src.shape[1]
+            view = dst.rearrange("p (q j) -> p q j", j=n)
+            again = src.unsqueeze(1).to_broadcast([P, q, n])
+            if by_dma:
+                nc.sync.dma_start(out=view, in_=again)
+            else:
+                nc.vector.tensor_copy(out=view, in_=again)
+
+        def x_tiles(b):
+            xin[b] = (ring.tile([P, IN1 + NB * BLK], U32, name="xinc", tag="xinc", align_bytes=64),
+                      ring.tile([P, IN1 + NB * BLK], U8, name="xins", tag="xins", align_bytes=64))
+            xout[b] = (ring.tile([P, L * TB], U32, name="xouc", tag="xouc", align_bytes=64),
+                       ring.tile([P, L * TB], U8, name="xous", tag="xous", align_bytes=64))
+
+        def x_inner_long(b):
+            for k, x in enumerate((xc, xs)):
+                spread(xin[b][k][:, 0:NCOL].bitcast(I32), x[:, L * b:L * (b + 1)].bitcast(I32), HT, b > 0)
+
+        def x_inner_blocks(b, c0=1, c1=NB):
+            m = c1 - c0
+            for k, x in enumerate((xc, xs)):
+                src = x[:, L * b + TB * c0:L * b + TB * c1].bitcast(I32)
+                n = src.shape[1] // m
+                dst = xin[b][k][:, IN1 + BLK * c0:IN1 + BLK * c1].bitcast(I32)
+                if b and k == 0:
+                    for c in range(m):
+                        spread(dst[:, n * TB * c:n * TB * (c + 1)], src[:, n * c:n * (c + 1)], TB, True)
+                else:
+                    nc.vector.tensor_copy(out=dst.rearrange("p (c q j) -> p c q j", c=m, q=TB),
+                                          in_=src.rearrange("p (c j) -> p c j", c=m).unsqueeze(2).to_broadcast([P, m, TB, n]))
+
+        def inner(b, n0, n):
+            return xin[b][0][:, n0:n0 + n], xin[b][1][:, n0:n0 + n]
+
+        def x_four(b):
             for q in range(4):
                 nc.vector.tensor_copy(out=x4s[:, 4 * L * b + q:4 * L * (b + 1):4], in_=xs[:, L * b:L * (b + 1)])
 
-        NX = L * TB
-
         def x_outer(b, c0=0, c1=NB):
-            n0, n1 = NX * b + BLK * c0, NX * b + BLK * c1
             t0, t1 = L * b + TB * c0, L * b + TB * c1
-            nc.vector.tensor_copy(
-                out=xfc[:, n0:n1].bitcast(I32).rearrange("p (r q) -> p r q", q=TB),
-                in_=xc[:, t0:t1].bitcast(I32).unsqueeze(2).to_broadcast([P, t1 - t0, TB]),
-            )
-            nc.vector.tensor_copy(
-                out=xfs[:, n0:n1].bitcast(I32).rearrange("p (r q) -> p r q", q=TB // 4),
-                in_=x4s[:, 4 * t0:4 * t1].bitcast(I32).unsqueeze(2).to_broadcast([P, t1 - t0, TB // 4]),
-            )
-
-        def x_inner(b, c0=0, c1=NB):
-            n0, n1 = NX * b + BLK * c0, NX * b + BLK * c1
-            t0, t1 = L * b + TB * c0, L * b + TB * c1
-            for dst, src_x in ((xsc, xc), (xss, xs)):
-                src = src_x[:, t0:t1].bitcast(I32).rearrange("p (c j) -> p c j", c=c1 - c0)
+            for k, (x, q) in enumerate(((xc[:, t0:t1], TB), (x4s[:, 4 * t0:4 * t1], TB // 4))):
                 nc.vector.tensor_copy(
-                    out=dst[:, n0:n1].bitcast(I32).rearrange("p (c q j) -> p c q j", c=c1 - c0, q=TB),
-                    in_=src.unsqueeze(2).to_broadcast([P, c1 - c0, TB, src.shape[2]]),
+                    out=xout[b][k][:, BLK * c0:BLK * c1].bitcast(I32).rearrange("p (r q) -> p r q", q=q),
+                    in_=x.bitcast(I32).unsqueeze(2).to_broadcast([P, t1 - t0, q]),
                 )
 
-        pidx = {}
-        for b in range(B):
-            for a in range(NB):
-                for c in range(a, NB):
-                    pidx[(b, a, c)] = len(pidx)
+        def outer(b, c):
+            return xout[b][0][:, BLK * c:BLK * (c + 1)], xout[b][1][:, BLK * c:BLK * (c + 1)]
 
-        def p_mul(b, a, c0, c1):
-            n = c1 - c0
-            pb = ring.tile([P, n, TB, TB, T], BF16, name="pb", tag="pb", align_bytes=64, bufs=3)
-            ta = L * b + TB * a
-            tcc = L * b + TB * c0
-            for k in range(n):
+        ROW0 = TB * L
+        BLOCKS = ((1, 2), (1, 3), (2, 2), (2, 3), (1, 1), (3, 3))
+        COPIES = ((0, 1), (0, 2), (0, 3))
+        PCOL = {ac: ROW0 + BLK * i for i, ac in enumerate(BLOCKS + COPIES)}
+        NPC = ROW0 + BLK * len(BLOCKS + COPIES)
+        pcodes = {}
+
+        def p_mul(b, j):
+            if b not in pcodes:
+                pcodes[b] = (ring.tile([P, NPC], U32, name="pc", tag="pc", align_bytes=64),
+                             ring.tile([P, NPC], U8, name="psc", tag="psc", align_bytes=64))
+            pb = ring.tile([P, NCOL, T], BF16, name="pb", tag="pb", align_bytes=64, bufs=3)
+            if j < 2:
+                parts = ((HT * j, HT, 0, L),)
+            else:
+                parts = tuple((TB * a, TB, TB * c, TB) for a, c in BLOCKS[2 * j - 4:2 * j - 2])
+            n0 = 0
+            for t0, nt, u0, nu in parts:
+                ta = L * b + t0
+                tu = L * b + u0
                 nc.vector.tensor_tensor(
-                    out=pb[:, k],
-                    in0=xg[:, ta:ta + TB, :].unsqueeze(2).to_broadcast([P, TB, TB, T]),
-                    in1=xg[:, tcc + TB * k:tcc + TB * (k + 1), :].unsqueeze(1).to_broadcast([P, TB, TB, T]),
+                    out=pb[:, n0:n0 + nt * nu, :].rearrange("p (i j) t -> p i j t", j=nu),
+                    in0=xg[:, ta:ta + nt, :].unsqueeze(2).to_broadcast([P, nt, nu, T]),
+                    in1=xg[:, tu:tu + nu, :].unsqueeze(1).to_broadcast([P, nt, nu, T]),
                     op=ALU.mult,
                 )
-            return (b, a, c0, c1, pb)
+                n0 += nt * nu
+            return (b, j, pb)
 
         def p_quant(job):
-            b, a, c0, c1, pb = job
-            c = c0
-            while c < c1:
-                n = 4 if c1 - c >= 4 else (2 if c1 - c >= 2 else 1)
-                i = pidx[(b, a, c)]
-                nc.vector.quantize_mx(
-                    out=pc[:, i:i + n, :].rearrange("p n w -> p (n w)").bitcast(FP8X4),
-                    scales=psc[:, i:i + n, :].rearrange("p n w -> p (n w)"),
-                    in_=pb[:, c - c0:c - c0 + n].rearrange("p c i j t -> p (c i j t)"),
+            b, j, pb = job
+            run = slice(NCOL * j, NCOL * (j + 1))
+            nc.vector.quantize_mx(out=pcodes[b][0][:, run].bitcast(FP8X4), scales=pcodes[b][1][:, run],
+                                  in_=pb[:].rearrange("p n t -> p (n t)"))
+
+        def p_copy(b):
+            for k in range(2):
+                words = pcodes[b][k][:].bitcast(I32)
+                n = words.shape[1]
+                nc.vector.tensor_copy(
+                    out=words[:, n * (NPC - 3 * BLK) // NPC:].rearrange("p (c i j) -> p c i j", c=3, i=TB),
+                    in_=words[:, 0:n * ROW0 // NPC].rearrange("p (i c j) -> p c i j", i=TB, c=NB)[:, 1:, :, :],
                 )
-                c += n
 
         def w_regroup(copy_fn, w, n0, n1):
             regroup(copy_fn, wg[w][:, n0:n1, :], wraw[w][:, :, n0:n1])
@@ -172,135 +204,170 @@ def tile_srlbertold_pa_t_kernel(tc, seq_out, W_proj, b_proj, W_out, b_out, out):
             nc.vector.quantize_mx(out=wc[w][:, n0:n1].bitcast(FP8X4), scales=ws[w][:, n0:n1],
                                   in_=wg[w][:, n0:n1, :].rearrange("p n t -> p (n t)"))
 
+        BLOCKPAIRS = {"dir1": ((1, 2), (1, 3)), "dir2": ((2, 2), (2, 3)), "mir0": ((2, 0), (3, 0)), "mir1": ((2, 1), (3, 1)),
+                      "mix1": ((1, 1), (1, 0)), "mix3": ((3, 3), (3, 2)), "end3": ((3, 3),), "end2": ((3, 2),)}
+        FIRST = ("dir1", "mir1", "row0a", "row0b", "mix1", "mir0", "dir2", "mix3")
+        LATER = ("row0a", "mir1", "row0b", "mix1", "dir1", "mir0", "dir2", "mix3")
+        units = [(b, k) for b in range(B) for k in (LATER if b else FIRST)]
+        units[-1:] = [(B - 1, "end3"), (B - 1, "end2")]
+        NU = len(units)
+        UB = len(FIRST)
+
+        def columns(u):
+            return BLK if units[u][1] in ("end3", "end2") else NCOL
+
+        def mx(o, w, t, codes, start, stop):
+            hs = slice(P * t, P * (t + 1))
+            nc.tensor.matmul_mx(out=o, lhsT=wc[w][:, hs].bitcast(FP8X4), lhsT_scale=ws[w][:, hs],
+                                rhs=codes[0].bitcast(FP8X4), rhs_scale=codes[1], start=start, stop=stop)
+
+        def pcols(b, n0, n):
+            return pcodes[b][0][:, n0:n0 + n], pcodes[b][1][:, n0:n0 + n]
+
+        def row0_mm(b, t, h):
+            bank = ps1.tile([P, NCOL], F32, name="bank", tag="s1")
+            mx(bank[:], 0, t, pcols(b, NCOL * h, NCOL), True, False)
+            mx(bank[:], 2, t, inner(b, 0, NCOL), False, True)
+            return bank
+
+        def row0_act(b, t, h, bank, pl):
+            for i in range(HT):
+                run = slice(L * i, L * (i + 1))
+                nc.scalar.activation(out=pl[:, t, run], in_=bank[:, run], func=ACT.Tanh,
+                                     bias=xbias[:, t, L * b + HT * h + i:L * b + HT * h + i + 1], scale=1.0)
+
+        def stage1(u, t, pl):
+            b, kind = units[u]
+            if kind in ("row0a", "row0b"):
+                h = 0 if kind == "row0a" else 1
+                row0_act(b, t, h, row0_mm(b, t, h), pl)
+                return
+            bank = ps1.tile([P, 2, BLK], F32, name="bank", tag="s1")
+            both = bank[:].rearrange("p e n -> p (e n)")
+            a0, c0 = BLOCKPAIRS[kind][0]
+            if kind in ("dir1", "dir2"):
+                mx(both, 0, t, pcols(b, PCOL[(a0, c0)], NCOL), True, False)
+                if u == 0 or t not in ECHUNKS:
+                    for e in range(2):
+                        mx(bank[:, e, :], 1, t, outer(b, a0), False, False)
+                mx(both, 2, t, inner(b, IN1 + BLK * c0, NCOL), False, True)
+                if u > 0 and t in ECHUNKS:
+                    for i in range(TB):
+                        tok = L * b + TB * a0 + i
+                        nc.scalar.activation(out=pl[:, t, :].rearrange("p (e i j) -> p e i j", e=2, i=TB)[:, :, i, :],
+                                             in_=bank[:, :, TB * i:TB * (i + 1)], func=ACT.Tanh,
+                                             bias=xbias[:, t, tok:tok + 1], scale=1.0)
+                    return
+            elif kind in ("mir0", "mir1"):
+                mx(both, 0, t, pcols(b, PCOL[(c0, a0)], NCOL), True, False)
+                for e in range(2):
+                    mx(bank[:, e, :], 2, t, outer(b, c0), False, False)
+                mx(both, 1, t, inner(b, IN1 + BLK * a0, NCOL), False, True)
+            else:
+                for e, (a, c) in enumerate(BLOCKPAIRS[kind]):
+                    out_token, in_token = (a, c) if a <= c else (c, a)
+                    wo, wi = (1, 2) if a <= c else (2, 1)
+                    mx(bank[:, e, :], 0, t, pcols(b, PCOL[(out_token, in_token)], BLK), True, False)
+                    mx(bank[:, e, :], wo, t, outer(b, out_token), False, False)
+                    mx(bank[:, e, :], wi, t, inner(b, IN1 + BLK * in_token, BLK), False, True)
+            nc.scalar.activation(out=pl[:, t, :], in_=both[:, 0:columns(u)], func=ACT.Tanh, bias=biasf[:, t:t + 1], scale=1.0)
+
+        def bias_mm(g, w, o, t):
+            mx(o, w, t, (xc[:, P * g:P * (g + 1)], xs[:, P * g:P * (g + 1)]), True, True)
+
+        def bias_copy(g, o, t):
+            nc.scalar.activation(out=xbias[:, t, P * g:P * (g + 1)], in_=o, func=ACT.Identity, bias=biasf[:, t:t + 1], scale=1.0)
+
+        def bias_terms(g):
+            xi = ps1.tile([P, T, P], F32, name="xi", tag="s1")
+            for t in range(T):
+                bias_mm(g, 1, xi[:, t, :], t)
+            for t in range(T):
+                bias_copy(g, xi[:, t, :], t)
+
+        def empty(kind, dst, view):
+            if kind in EMPTIED_BY_VECTOR:
+                nc.vector.tensor_scalar(out=dst, in0=view, scalar1=biasf[:, 4:5], scalar2=None, op0=ALU.add)
+            else:
+                nc.scalar.activation(out=dst, in_=view, func=ACT.Identity, bias=biasf[:, 4:5], scale=1.0)
+
+        def store(b, r0, r1, ost):
+            nc.sync.dma_start(out=out[b, :, r0:r1, :].rearrange("k f s -> k (f s)"),
+                              in_=ost[:, r0:r1, :].rearrange("p f s -> p (f s)"))
+
+        def stage2(u, qc, qs, ost):
+            b, kind = units[u]
+            bank2 = ps2.tile([P, NCOL], F32, name="bank2", tag="s2")
+            nc.tensor.matmul_mx(out=bank2[:, 0:columns(u)], lhsT=woc[:].bitcast(FP8X4), lhsT_scale=wos[:],
+                                rhs=qc[:].bitcast(FP8X4), rhs_scale=qs[:], start=True, stop=True)
+            if kind in ("row0a", "row0b"):
+                t0 = 0 if kind == "row0a" else HT
+                empty(kind, ost[:, t0:t0 + HT, :], bank2[:].rearrange("p (f s) -> p f s", s=L))
+                if kind == "row0b":
+                    store(b, 0, TB, ost)
+                return
+            a0, c0 = BLOCKPAIRS[kind][0]
+            if kind in ("dir1", "dir2"):
+                empty(kind, ost[:, TB * a0:TB * (a0 + 1), TB * c0:TB * (c0 + 2)].rearrange("p f (e s) -> p f e s", e=2),
+                      bank2[:].rearrange("p (e f s) -> p f e s", e=2, f=TB))
+            elif kind in ("mir0", "mir1"):
+                empty(kind, ost[:, TB * a0:TB * (a0 + 2), TB * c0:TB * (c0 + 1)].rearrange("p (e f) s -> p e f s", e=2),
+                      bank2[:].rearrange("p (e s f) -> p e f s", e=2, s=TB))
+            else:
+                for e, (a, c) in enumerate(BLOCKPAIRS[kind]):
+                    blk = bank2[:, BLK * e:BLK * (e + 1)]
+                    view = blk.rearrange("p (f s) -> p f s", f=TB) if a <= c else blk.rearrange("p (s f) -> p f s", s=TB)
+                    for h in range(2 if kind == "end2" else 1):
+                        f0, f1 = (HT * h, HT * (h + 1)) if kind == "end2" else (0, TB)
+                        empty(kind, ost[:, TB * a + f0:TB * a + f1, TB * c:TB * (c + 1)], view[:, f0:f1, :])
+                        if kind == "end2":
+                            store(b, TB * a + f0, TB * a + f1, ost)
+            whole = (STORES if b else STORES0).get(kind)
+            if whole is not None:
+                store(b, TB * whole, TB * (whole + 1), ost)
+
+        STORES = {"dir1": 1, "dir2": 2, "mix3": 3}
+        STORES0 = {"mix1": 1, "dir2": 2, "mix3": 3}
+
         PIECES = tuple((P * t, P * (t + 1)) for t in range(T))
         xt0 = x_transpose(0)
         bps = ps1.tile([P, P], BF16, name="bps", tag="s1")
         nc.tensor.transpose(bps[:], brows[:], ident[:])
-        for w in range(3):
-            w_regroup(nc.scalar.copy, w, *PIECES[0])
-        for piece in PIECES[1:]:
-            for w in range(2):
-                w_regroup(nc.scalar.copy, w, *piece)
+        for n0, n1 in PIECES[:2]:
+            for w in (0, 2, 1):
+                w_regroup(nc.scalar.copy, w, n0, n1)
         x_copy(0, xt0, 0, 1)
-        job0 = p_mul(0, 0, 0, 2)
+        job2 = p_mul(0, 2)
         x_copy(0, xt0, 1, 2)
-        p_quant(job0)
+        p_quant(job2)
         w_quant(0, *PIECES[0])
         quant_x(0)
         w_quant(1, *PIECES[0])
-        x_rep_four(0)
+        x_four(0)
         w_quant(2, *PIECES[0])
-        x_outer(0, 0, 1)
-        x_inner(0, 0, 2)
+        x_tiles(0)
+        x_outer(0, 1, 2)
+        x_inner_blocks(0, 2, 4)
         nc.vector.tensor_copy(out=biasf[:], in_=bps[:, 0:8])
-        w_regroup(nc.vector.tensor_copy, 2, *PIECES[1])
-        for w in range(3):
+        for w in (0, 2, 1):
             w_quant(w, *PIECES[1])
-        x_inner(0, 2, 4)
-        job1 = p_mul(0, 0, 2, 4)
-        for n0, n1 in PIECES[2:]:
-            w_regroup(nc.vector.tensor_copy, 2, n0, n1)
-            w_quant(0, n0, n1)
-            w_quant(1, n0, n1)
-            w_quant(2, n0, n1)
+        for piece in PIECES[2:]:
+            for w in (0, 2, 1):
+                w_regroup(nc.vector.tensor_copy, w, *piece)
+            for w in (0, 2, 1):
+                w_quant(w, *piece)
+        job0 = p_mul(0, 0)
+        x_inner_long(0)
+        p_quant(job0)
+        job1 = p_mul(0, 1)
+        x_outer(0, 0, 1)
+        x_inner_blocks(0, 1, 2)
         p_quant(job1)
-        x_outer(0, 1, 4)
-        job2 = p_mul(0, 1, 1, 4)
+        x_outer(0, 2, 4)
         wog = keep.tile([P, P, T], BF16, name="wog", align_bytes=64)
-        p_quant(job2)
 
-        units = []
-        for b in range(B):
-            for a in range(NB):
-                units.append((b, a, 0, 2))
-                if (b, a) == (B - 1, NB - 1):
-                    units.append((b, a, 2, 1))
-                    units.append((b, a, 3, 1))
-                else:
-                    units.append((b, a, 2, 2))
-        NU = len(units)
-
-        def mx(o, w, t, rc, rs, start, stop):
-            hs = slice(P * t, P * (t + 1))
-            nc.tensor.matmul_mx(out=o, lhsT=wc[w][:, hs].bitcast(FP8X4), lhsT_scale=ws[w][:, hs],
-                                rhs=rc.bitcast(FP8X4), rhs_scale=rs, start=start, stop=stop)
-
-        def stage1(u, t, pl):
-            b, a, c0, n = units[u]
-            bank = ps1.tile([P, n * BLK], F32, name="bank", tag="s1")
-            if t in ECHUNKS and a <= c0 and n == 2 and u >= 1:
-                i0 = pidx[(b, a, c0)]
-                sc2 = slice(BLK * (NB * b + c0), BLK * (NB * b + c0 + 2))
-                mx(bank[:], 0, t, pc[:, i0:i0 + 2, :].rearrange("p n w -> p (n w)"),
-                   psc[:, i0:i0 + 2, :].rearrange("p n w -> p (n w)"), True, False)
-                mx(bank[:], 2, t, xsc[:, sc2], xss[:, sc2], False, True)
-                k = ECHUNKS.index(t)
-                for i in range(TB):
-                    tok = L * b + TB * a + i
-                    nc.scalar.activation(out=pl[:, t, :].rearrange("p (e i j) -> p e i j", e=2, i=TB)[:, :, i, :],
-                                         in_=bank[:].rearrange("p (e i j) -> p e i j", e=2, i=TB)[:, :, i, :],
-                                         func=ACT.Tanh, bias=xib[:, k, tok:tok + 1], scale=1.0)
-                return
-            if n == 2 and a <= c0:
-                i0 = pidx[(b, a, c0)]
-                sa = slice(BLK * (NB * b + a), BLK * (NB * b + a + 1))
-                sc2 = slice(BLK * (NB * b + c0), BLK * (NB * b + c0 + 2))
-                mx(bank[:], 0, t, pc[:, i0:i0 + 2, :].rearrange("p n w -> p (n w)"),
-                   psc[:, i0:i0 + 2, :].rearrange("p n w -> p (n w)"), True, False)
-                mx(bank[:, 0:BLK], 1, t, xfc[:, sa], xfs[:, sa], False, False)
-                mx(bank[:, BLK:], 1, t, xfc[:, sa], xfs[:, sa], False, False)
-                mx(bank[:], 2, t, xsc[:, sc2], xss[:, sc2], False, True)
-            for e in range(n if n == 1 or a > c0 else 0):
-                c = c0 + e
-                o = bank[:, BLK * e:BLK * (e + 1)]
-                i = pidx[(b, min(a, c), max(a, c))]
-                sa = slice(BLK * (NB * b + a), BLK * (NB * b + a + 1))
-                scc = slice(BLK * (NB * b + c), BLK * (NB * b + c + 1))
-                mx(o, 0, t, pc[:, i, :], psc[:, i, :], True, False)
-                if a <= c:
-                    mx(o, 1, t, xfc[:, sa], xfs[:, sa], False, False)
-                    mx(o, 2, t, xsc[:, scc], xss[:, scc], False, True)
-                else:
-                    mx(o, 1, t, xsc[:, sa], xss[:, sa], False, False)
-                    mx(o, 2, t, xfc[:, scc], xfs[:, scc], False, True)
-            nc.scalar.activation(out=pl[:, t, :], in_=bank[:], func=ACT.Tanh, bias=biasf[:, t:t + 1], scale=1.0)
-
-        def first_term(g):
-            xi = ps1.tile([P, len(ECHUNKS), P], F32, name="xi", tag="s1")
-            for k in range(len(ECHUNKS)):
-                mx(xi[:, k, :], 1, ECHUNKS[k], xc[:, P * g:P * (g + 1)], xs[:, P * g:P * (g + 1)], True, True)
-            for k in range(len(ECHUNKS)):
-                nc.scalar.activation(out=xib[:, k, P * g:P * (g + 1)], in_=xi[:, k, :], func=ACT.Identity,
-                                     bias=biasf[:, ECHUNKS[k]:ECHUNKS[k] + 1], scale=1.0)
-
-        def stage2(u, qc, qs, ost):
-            b, a, c0, n = units[u]
-            bank2 = ps2.tile([P, n * BLK], F32, name="bank2", tag="s2")
-            nc.tensor.matmul_mx(out=bank2[:], lhsT=woc[:].bitcast(FP8X4), lhsT_scale=wos[:],
-                                rhs=qc[:].bitcast(FP8X4), rhs_scale=qs[:], start=True, stop=True)
-            if n == 2 and (a <= c0 or a > c0 + 1):
-                if a <= c0:
-                    view = bank2[:].rearrange("p (e f s) -> p f e s", e=2, f=TB)
-                else:
-                    view = bank2[:].rearrange("p (e s f) -> p f e s", e=2, s=TB)
-                dst = ost[:, :, TB * c0:TB * (c0 + 2)].rearrange("p f (e s) -> p f e s", e=2)
-                if u % 4 == 0:
-                    nc.vector.tensor_scalar(out=dst, in0=view, scalar1=biasf[:, 4:5], scalar2=None, op0=ALU.add)
-                else:
-                    nc.scalar.activation(out=dst, in_=view, func=ACT.Identity, bias=biasf[:, 4:5], scale=1.0)
-            else:
-                for e in range(n):
-                    c = c0 + e
-                    blk = bank2[:, BLK * e:BLK * (e + 1)]
-                    if a <= c:
-                        view = blk.rearrange("p (f s) -> p f s", f=TB)
-                    else:
-                        view = blk.rearrange("p (s f) -> p f s", s=TB)
-                    nc.scalar.activation(out=ost[:, :, TB * c:TB * (c + 1)], in_=view, func=ACT.Identity,
-                                         bias=biasf[:, 4:5], scale=1.0)
-            if c0 + n == NB:
-                nc.sync.dma_start(out=out[b, :, TB * a:TB * (a + 1), :].rearrange("k f s -> k (f s)"),
-                                  in_=ost[:].rearrange("p f s -> p (f s)"))
+        PJOBS = {0: (0, 3), 3: (1, 0), 4: (1, 2), 5: (1, 1), 6: (1, 4)}
+        PJOBS0 = {0: (0, 4), 2: (0, 3), 3: (1, 0), 4: (1, 2), 5: (1, 1), 6: (1, 4)}
 
         planes = {}
         codes = {}
@@ -309,44 +376,50 @@ def tile_srlbertold_pa_t_kernel(tc, seq_out, W_proj, b_proj, W_out, b_out, out):
         for s in range(NU + LAGD):
             u2 = s - LAGD
             if u2 >= 0:
-                row = units[u2][0:2]
-                if units[u2][2] == 0:
-                    ostage[row] = ring.tile([P, TB, L], F32, name="ost", tag="ost", bufs=3)
-                stage2(u2, codes[u2][0], codes[u2][1], ostage[row])
-            if s == 1 or s == 2 * NB + 1:
-                first_term(s // (2 * NB))
+                b2 = units[u2][0]
+                if b2 not in ostage:
+                    ostage[b2] = ring.tile([P, L, L], F32, name="ost", tag="ost")
+                stage2(u2, codes[u2][0], codes[u2][1], ostage[b2])
             if s < NU:
-                planes[s] = ring.tile([P, T, units[s][3] * BLK], BF16, name="pl", tag="pl", bufs=LAGD + 1)
+                planes[s] = ring.tile([P, T, columns(s)], BF16, name="pl", tag="pl", bufs=5)
+                if s == 1:
+                    bias_terms(0)
+                if s == 2 * UB - 2:
+                    bias_terms(1)
                 for t in range(T):
                     stage1(s, t, planes[s])
-            if s == 1:
-                regroup(nc.scalar.copy, wog[:], woraw[:])
+                if s == 1:
+                    regroup(nc.scalar.copy, wog[:], woraw[:])
             u1 = s - 1
             if 0 <= u1 < NU:
-                n1 = units[u1][3] * BLK
-                g2 = ring.tile([P, n1, T], BF16, name="g2", tag="g2", align_bytes=64, bufs=3)
+                g2 = ring.tile([P, columns(u1), T], BF16, name="g2", tag="g2", align_bytes=64, bufs=3)
                 regroup(nc.vector.tensor_copy, g2[:], planes[u1][:])
             for job in pending:
                 p_quant(job)
             pending = []
-            r = s + PLEAD
-            if r < NU and units[r][2] == 0:
-                pending.append(p_mul(units[r][0], units[r][1], units[r][1], NB))
-            if 0 <= u1 < NU:
-                qc = ring.tile([P, n1], U32, name="qc", tag="qc", align_bytes=64, bufs=LAGD + 2)
-                qs = ring.tile([P, n1], U8, name="qs", tag="qs", align_bytes=64, bufs=LAGD + 2)
-                nc.vector.quantize_mx(out=qc[:].bitcast(FP8X4), scales=qs[:], in_=g2[:].rearrange("p n t -> p (n t)"))
-                codes[u1] = (qc, qs)
+            b, r = divmod(s, UB)
+            table = PJOBS if b else PJOBS0
+            if r in table and b + table[r][0] < B:
+                pending.append(p_mul(b + table[r][0], table[r][1]))
+            if s == 0:
+                p_copy(0)
             if s == 2:
                 nc.vector.quantize_mx(out=woc[:].bitcast(FP8X4), scales=wos[:], in_=wog[:].rearrange("p n t -> p (n t)"))
                 x_copy(1, x_transpose(1), 2, 4)
             if s == 4:
                 quant_x(1)
-            nb = s // (2 * NB) + 1
-            if nb < B:
-                if s % (2 * NB) == 1:
-                    x_inner(nb)
-                if s % (2 * NB) == 3:
-                    x_rep_four(nb)
-                if s % (2 * NB) == 5:
-                    x_outer(nb)
+            if b + 1 < B:
+                if r == 1:
+                    x_tiles(b + 1)
+                    x_four(b + 1)
+                    x_inner_long(b + 1)
+                if r == 2:
+                    x_outer(b + 1)
+                    x_inner_blocks(b + 1)
+                if r == 7:
+                    p_copy(b + 1)
+            if 0 <= u1 < NU:
+                qc = ring.tile([P, columns(u1)], U32, name="qc", tag="qc", align_bytes=64, bufs=LAGD + 2)
+                qs = ring.tile([P, columns(u1)], U8, name="qs", tag="qs", align_bytes=64, bufs=LAGD + 2)
+                nc.vector.quantize_mx(out=qc[:].bitcast(FP8X4), scales=qs[:], in_=g2[:].rearrange("p n t -> p (n t)"))
+                codes[u1] = (qc, qs)

@@ -25,7 +25,7 @@ BLK = TB * TB
 HT = TB // 2
 HB = BLK // 2
 ECHUNKS = (1, 2, 3)
-EMPTIED_BY_VECTOR = ("row0a",)
+EMPTIED_BY_VECTOR = ()
 LAGD = 5
 
 
@@ -120,7 +120,7 @@ def tile_srlbertold_pa_t_kernel(tc, seq_out, W_proj, b_proj, W_out, b_out, out):
 
         def x_inner_long(b):
             for k, x in enumerate((xc, xs)):
-                spread(xin[b][k][:, 0:NCOL].bitcast(I32), x[:, L * b:L * (b + 1)].bitcast(I32), HT, b > 0)
+                spread(xin[b][k][:, 0:NCOL].bitcast(I32), x[:, L * b:L * (b + 1)].bitcast(I32), HT, False)
 
         def x_inner_blocks(b, c0=1, c1=NB):
             m = c1 - c0
@@ -128,7 +128,7 @@ def tile_srlbertold_pa_t_kernel(tc, seq_out, W_proj, b_proj, W_out, b_out, out):
                 src = x[:, L * b + TB * c0:L * b + TB * c1].bitcast(I32)
                 n = src.shape[1] // m
                 dst = xin[b][k][:, IN1 + BLK * c0:IN1 + BLK * c1].bitcast(I32)
-                if b and k == 0:
+                if False:
                     for c in range(m):
                         spread(dst[:, n * TB * c:n * TB * (c + 1)], src[:, n * c:n * (c + 1)], TB, True)
                 else:
@@ -138,9 +138,9 @@ def tile_srlbertold_pa_t_kernel(tc, seq_out, W_proj, b_proj, W_out, b_out, out):
         def inner(b, n0, n):
             return xin[b][0][:, n0:n0 + n], xin[b][1][:, n0:n0 + n]
 
-        def x_four(b):
+        def x_four(b, m):
             for q in range(4):
-                nc.vector.tensor_copy(out=x4s[:, 4 * L * b + q:4 * L * (b + 1):4], in_=xs[:, L * b:L * (b + 1)])
+                nc.vector.tensor_copy(out=x4s[:, 4 * L * b + q:4 * L * (b + m):4], in_=xs[:, L * b:L * (b + m)])
 
         def x_outer(b, c0=0, c1=NB):
             t0, t1 = L * b + TB * c0, L * b + TB * c1
@@ -343,7 +343,7 @@ def tile_srlbertold_pa_t_kernel(tc, seq_out, W_proj, b_proj, W_out, b_out, out):
         w_quant(0, *PIECES[0])
         quant_x(0)
         w_quant(1, *PIECES[0])
-        x_four(0)
+        x_four(0, 1)
         w_quant(2, *PIECES[0])
         x_tiles(0)
         x_outer(0, 1, 2)
@@ -411,10 +411,12 @@ def tile_srlbertold_pa_t_kernel(tc, seq_out, W_proj, b_proj, W_out, b_out, out):
             if b + 1 < B:
                 if r == 1:
                     x_tiles(b + 1)
-                    x_four(b + 1)
+                    if b < 2:
+                        x_four(b + 1, b + 1)
                     x_inner_long(b + 1)
                 if r == 2:
                     x_outer(b + 1)
+                if r == 3:
                     x_inner_blocks(b + 1)
                 if r == 7:
                     p_copy(b + 1)

from contextlib import ExitStack

import concourse.mybir as mybir
from concourse.masks import make_identity

FLOPS = 2 * 16384 * 512 * 512 + 2 * 2 * 256 * 512 * 512 + 2 * 16384 * 512 * 128

BF16 = mybir.dt.bfloat16
F32 = mybir.dt.float32
U32 = mybir.dt.uint32
U8 = mybir.dt.uint8
I32 = mybir.dt.int32
FP8X4 = mybir.dt.float8_e4m3fn_x4
ACT = mybir.ActivationFunctionType
ALU = mybir.AluOpType

P = 128
B = 4
L = 64
H = 512
T = 4
TB = 16
NB = L // TB
BLK = TB * TB
HT = TB // 2
HB = BLK // 2
ECHUNKS = (1, 2, 3)
EMPTIED_BY_VECTOR = ()
LAGD = 5


def regroup(engine_copy, dst, src):
    engine_copy(
        out=dst.rearrange("p (c i) t -> p c t i", i=8),
        in_=src.rearrange("p t (c i) -> p c t i", i=8),
    )


def tile_srlbertold_pa_t_kernel(tc, seq_out, W_proj, b_proj, W_out, b_out, out):
    nc = tc.nc
    with ExitStack() as ctx:
        ctx.enter_context(tc.manual_schedule())
        keep = ctx.enter_context(tc.tile_pool(name="keep", bufs=1))
        ring = ctx.enter_context(tc.tile_pool(name="ring", bufs=2))
        ps1 = ctx.enter_context(tc.psum_pool(name="ps1", bufs=5))
        ps2 = ctx.enter_context(tc.psum_pool(name="ps2", bufs=3))

        x_sb = keep.tile([P, 2, H], BF16, name="x_sb")
        x_rows = seq_out.rearrange("b l h -> (b l) h").rearrange("(g p) h -> p g h", p=P)
        nc.sync.dma_start(out=x_sb[:, 0, :], in_=x_rows[:, 0, :])
        brows = keep.tile([P, P], BF16, name="brows")
        nc.vector.memset(brows[:], 0.0)
        nc.sync.dma_start(out=brows[0:4, :], in_=b_proj.rearrange("(t p) -> t p", p=P))
        nc.sync.dma_start(out=brows[4:5, :], in_=b_out.rearrange("(o k) -> o k", o=1))
        wraw = {}
        for w in (0, 2, 1):
            wraw[w] = keep.tile([P, T, H], BF16, name="wraw%d" % w)
        for n0, n1 in ((0, P), (P, H)):
            for w in (0, 2, 1):
                nc.sync.dma_start(out=wraw[w][:, :, n0:n1], in_=W_proj[H * w:H * (w + 1), n0:n1].rearrange("(t p) n -> p t n", p=P))
        nc.sync.dma_start(out=x_sb[:, 1, :], in_=x_rows[:, 1, :])
        woraw = keep.tile([P, T, P], BF16, name="woraw")
        nc.sync.dma_start(out=woraw[:], in_=W_out.rearrange("(t p) n -> p t n", p=P))

        ident = keep.tile([P, P], BF16, name="ident")
        make_identity(nc, ident[:])

        warm = keep.tile([P, 1], F32, name="warm")
        nc.vector.memset(warm[:], 0.0)
        nc.scalar.activation(out=warm[:], in_=warm[:], func=ACT.Tanh)

        xg = keep.tile([P, B * L, T], BF16, name="xg", align_bytes=64)
        xc = keep.tile([P, B * L], U32, name="xc", align_bytes=64)
        xs = keep.tile([P, B * L], U8, name="xs", align_bytes=64)
        nc.vector.memset(xs[:].bitcast(I32), 0)
        x4s = keep.tile([P, B * L * 4], U8, name="x4s", align_bytes=64)
        wg = [keep.tile([P, H, T], BF16, name="wg%d" % w, align_bytes=64) for w in range(3)]
        wc = [keep.tile([P, H], U32, name="wc%d" % w, align_bytes=64) for w in range(3)]
        ws = [keep.tile([P, H], U8, name="ws%d" % w, align_bytes=64) for w in range(3)]
        woc = keep.tile([P, P], U32, name="woc", align_bytes=64)
        wos = keep.tile([P, P], U8, name="wos", align_bytes=64)
        biasf = keep.tile([P, 8], F32, name="biasf")
        xbias = keep.tile([P, T, B * L], F32, name="xbias")

        def x_transpose(g):
            xt = ps2.tile([P, T, P], BF16, name="xt", tag="s2")
            for t in range(T):
                nc.tensor.transpose(xt[:, t, :], x_sb[:, g, P * t:P * (t + 1)], ident[:])
            return xt

        def x_copy(g, xt, b0, b1):
            nc.vector.tensor_copy(out=xg[:, L * b0:L * b1, :], in_=xt[:, :, L * b0 - P * g:L * b1 - P * g].rearrange("p t r -> p r t"))

        def quant_x(g):
            nc.vector.quantize_mx(
                out=xc[:, P * g:P * (g + 1)].bitcast(FP8X4),
                scales=xs[:, P * g:P * (g + 1)],
                in_=xg[:, P * g:P * (g + 1), :].rearrange("p r t -> p (r t)"),
            )

        NCOL = 2 * BLK
        IN1 = NCOL - BLK
        xin = {}
        xout = {}

        def spread(dst, src, q, by_dma):
            n = src.shape[1]
            view = dst.rearrange("p (q j) -> p q j", j=n)
            again = src.unsqueeze(1).to_broadcast([P, q, n])
            if by_dma:
                nc.sync.dma_start(out=view, in_=again)
            else:
                nc.vector.tensor_copy(out=view, in_=again)

        def x_tiles(b):
            xin[b] = (ring.tile([P, IN1 + NB * BLK], U32, name="xinc", tag="xinc", align_bytes=64),
                      ring.tile([P, IN1 + NB * BLK], U8, name="xins", tag="xins", align_bytes=64))
            xout[b] = (ring.tile([P, L * TB], U32, name="xouc", tag="xouc", align_bytes=64),
                       ring.tile([P, L * TB], U8, name="xous", tag="xous", align_bytes=64))

        def x_inner_long(b):
            for k, x in enumerate((xc, xs)):
                spread(xin[b][k][:, 0:NCOL].bitcast(I32), x[:, L * b:L * (b + 1)].bitcast(I32), HT, False)

        def x_inner_blocks(b, c0=1, c1=NB):
            m = c1 - c0
            for k, x in enumerate((xc, xs)):
                src = x[:, L * b + TB * c0:L * b + TB * c1].bitcast(I32)
                n = src.shape[1] // m
                dst = xin[b][k][:, IN1 + BLK * c0:IN1 + BLK * c1].bitcast(I32)
                if False:
                    for c in range(m):
                        spread(dst[:, n * TB * c:n * TB * (c + 1)], src[:, n * c:n * (c + 1)], TB, True)
                else:
                    nc.vector.tensor_copy(out=dst.rearrange("p (c q j) -> p c q j", c=m, q=TB),
                                          in_=src.rearrange("p (c j) -> p c j", c=m).unsqueeze(2).to_broadcast([P, m, TB, n]))

        def inner(b, n0, n):
            return xin[b][0][:, n0:n0 + n], xin[b][1][:, n0:n0 + n]

        def x_four(b, m):
            for q in range(4):
                nc.vector.tensor_copy(out=x4s[:, 4 * L * b + q:4 * L * (b + m):4], in_=xs[:, L * b:L * (b + m)])

        def x_outer(b, c0=0, c1=NB):
            t0, t1 = L * b + TB * c0, L * b + TB * c1
            for k, (x, q) in enumerate(((xc[:, t0:t1], TB), (x4s[:, 4 * t0:4 * t1], TB // 4))):
                nc.vector.tensor_copy(
                    out=xout[b][k][:, BLK * c0:BLK * c1].bitcast(I32).rearrange("p (r q) -> p r q", q=q),
                    in_=x.bitcast(I32).unsqueeze(2).to_broadcast([P, t1 - t0, q]),
                )

        def outer(b, c):
            return xout[b][0][:, BLK * c:BLK * (c + 1)], xout[b][1][:, BLK * c:BLK * (c + 1)]

        ROW0 = TB * L
        BLOCKS = ((1, 2), (1, 3), (2, 2), (2, 3), (1, 1), (3, 3))
        COPIES = ((0, 1), (0, 2), (0, 3))
        PCOL = {ac: ROW0 + BLK * i for i, ac in enumerate(BLOCKS + COPIES)}
        NPC = ROW0 + BLK * len(BLOCKS + COPIES)
        pcodes = {}

        def p_mul(b, j):
            if b not in pcodes:
                pcodes[b] = (ring.tile([P, NPC], U32, name="pc", tag="pc", align_bytes=64),
                             ring.tile([P, NPC], U8, name="psc", tag="psc", align_bytes=64))
            pb = ring.tile([P, NCOL, T], BF16, name="pb", tag="pb", align_bytes=64, bufs=3)
            if j < 2:
                parts = ((HT * j, HT, 0, L),)
            else:
                parts = tuple((TB * a, TB, TB * c, TB) for a, c in BLOCKS[2 * j - 4:2 * j - 2])
            n0 = 0
            for t0, nt, u0, nu in parts:
                ta = L * b + t0
                tu = L * b + u0
                nc.vector.tensor_tensor(
                    out=pb[:, n0:n0 + nt * nu, :].rearrange("p (i j) t -> p i j t", j=nu),
                    in0=xg[:, ta:ta + nt, :].unsqueeze(2).to_broadcast([P, nt, nu, T]),
                    in1=xg[:, tu:tu + nu, :].unsqueeze(1).to_broadcast([P, nt, nu, T]),
                    op=ALU.mult,
                )
                n0 += nt * nu
            return (b, j, pb)

        def p_quant(job):
            b, j, pb = job
            run = slice(NCOL * j, NCOL * (j + 1))
            nc.vector.quantize_mx(out=pcodes[b][0][:, run].bitcast(FP8X4), scales=pcodes[b][1][:, run],
                                  in_=pb[:].rearrange("p n t -> p (n t)"))

        def p_copy(b):
            for k in range(2):
                words = pcodes[b][k][:].bitcast(I32)
                n = words.shape[1]
                nc.vector.tensor_copy(
                    out=words[:, n * (NPC - 3 * BLK) // NPC:].rearrange("p (c i j) -> p c i j", c=3, i=TB),
                    in_=words[:, 0:n * ROW0 // NPC].rearrange("p (i c j) -> p c i j", i=TB, c=NB)[:, 1:, :, :],
                )

        def w_regroup(copy_fn, w, n0, n1):
            regroup(copy_fn, wg[w][:, n0:n1, :], wraw[w][:, :, n0:n1])

        def w_quant(w, n0, n1):
            nc.vector.quantize_mx(out=wc[w][:, n0:n1].bitcast(FP8X4), scales=ws[w][:, n0:n1],
                                  in_=wg[w][:, n0:n1, :].rearrange("p n t -> p (n t)"))

        BLOCKPAIRS = {"dir1": ((1, 2), (1, 3)), "dir2": ((2, 2), (2, 3)), "mir0": ((2, 0), (3, 0)), "mir1": ((2, 1), (3, 1)),
                      "mix1": ((1, 1), (1, 0)), "mix3": ((3, 3), (3, 2)), "end3": ((3, 3),), "end2": ((3, 2),)}
        FIRST = ("dir1", "mir1", "row0a", "row0b", "mix1", "mir0", "dir2", "mix3")
        LATER = ("row0a", "mir1", "row0b", "mix1", "dir1", "mir0", "dir2", "mix3")
        units = [(b, k) for b in range(B) for k in (LATER if b else FIRST)]
        units[-1:] = [(B - 1, "end3"), (B - 1, "end2")]
        NU = len(units)
        UB = len(FIRST)

        def columns(u):
            return BLK if units[u][1] in ("end3", "end2") else NCOL

        def mx(o, w, t, codes, start, stop):
            hs = slice(P * t, P * (t + 1))
            nc.tensor.matmul_mx(out=o, lhsT=wc[w][:, hs].bitcast(FP8X4), lhsT_scale=ws[w][:, hs],
                                rhs=codes[0].bitcast(FP8X4), rhs_scale=codes[1], start=start, stop=stop)

        def pcols(b, n0, n):
            return pcodes[b][0][:, n0:n0 + n], pcodes[b][1][:, n0:n0 + n]

        def row0_mm(b, t, h):
            bank = ps1.tile([P, NCOL], F32, name="bank", tag="s1")
            mx(bank[:], 0, t, pcols(b, NCOL * h, NCOL), True, False)
            mx(bank[:], 2, t, inner(b, 0, NCOL), False, True)
            return bank

        def row0_act(b, t, h, bank, pl):
            for i in range(HT):
                run = slice(L * i, L * (i + 1))
                nc.scalar.activation(out=pl[:, t, run], in_=bank[:, run], func=ACT.Tanh,
                                     bias=xbias[:, t, L * b + HT * h + i:L * b + HT * h + i + 1], scale=1.0)

        def stage1(u, t, pl):
            b, kind = units[u]
            if kind in ("row0a", "row0b"):
                h = 0 if kind == "row0a" else 1
                row0_act(b, t, h, row0_mm(b, t, h), pl)
                return
            bank = ps1.tile([P, 2, BLK], F32, name="bank", tag="s1")
            both = bank[:].rearrange("p e n -> p (e n)")
            a0, c0 = BLOCKPAIRS[kind][0]
            if kind in ("dir1", "dir2"):
                mx(both, 0, t, pcols(b, PCOL[(a0, c0)], NCOL), True, False)
                if u == 0 or t not in ECHUNKS:
                    for e in range(2):
                        mx(bank[:, e, :], 1, t, outer(b, a0), False, False)
                mx(both, 2, t, inner(b, IN1 + BLK * c0, NCOL), False, True)
                if u > 0 and t in ECHUNKS:
                    for i in range(TB):
                        tok = L * b + TB * a0 + i
                        nc.scalar.activation(out=pl[:, t, :].rearrange("p (e i j) -> p e i j", e=2, i=TB)[:, :, i, :],
                                             in_=bank[:, :, TB * i:TB * (i + 1)], func=ACT.Tanh,
                                             bias=xbias[:, t, tok:tok + 1], scale=1.0)
                    return
            elif kind in ("mir0", "mir1"):
                mx(both, 0, t, pcols(b, PCOL[(c0, a0)], NCOL), True, False)
                for e in range(2):
                    mx(bank[:, e, :], 2, t, outer(b, c0), False, False)
                mx(both, 1, t, inner(b, IN1 + BLK * a0, NCOL), False, True)
            else:
                for e, (a, c) in enumerate(BLOCKPAIRS[kind]):
                    out_token, in_token = (a, c) if a <= c else (c, a)
                    wo, wi = (1, 2) if a <= c else (2, 1)
                    mx(bank[:, e, :], 0, t, pcols(b, PCOL[(out_token, in_token)], BLK), True, False)
                    mx(bank[:, e, :], wo, t, outer(b, out_token), False, False)
                    mx(bank[:, e, :], wi, t, inner(b, IN1 + BLK * in_token, BLK), False, True)
            nc.scalar.activation(out=pl[:, t, :], in_=both[:, 0:columns(u)], func=ACT.Tanh, bias=biasf[:, t:t + 1], scale=1.0)

        def bias_mm(g, w, o, t):
            mx(o, w, t, (xc[:, P * g:P * (g + 1)], xs[:, P * g:P * (g + 1)]), True, True)

        def bias_copy(g, o, t):
            nc.scalar.activation(out=xbias[:, t, P * g:P * (g + 1)], in_=o, func=ACT.Identity, bias=biasf[:, t:t + 1], scale=1.0)

        def bias_terms(g):
            xi = ps1.tile([P, T, P], F32, name="xi", tag="s1")
            for t in range(T):
                bias_mm(g, 1, xi[:, t, :], t)
            for t in range(T):
                bias_copy(g, xi[:, t, :], t)

        def empty(kind, dst, view):
            if kind in EMPTIED_BY_VECTOR:
                nc.vector.tensor_scalar(out=dst, in0=view, scalar1=biasf[:, 4:5], scalar2=None, op0=ALU.add)
            else:
                nc.scalar.activation(out=dst, in_=view, func=ACT.Identity, bias=biasf[:, 4:5], scale=1.0)

        def store(b, r0, r1, ost):
            nc.sync.dma_start(out=out[b, :, r0:r1, :].rearrange("k f s -> k (f s)"),
                              in_=ost[:, r0:r1, :].rearrange("p f s -> p (f s)"))

        def stage2(u, qc, qs, ost):
            b, kind = units[u]
            bank2 = ps2.tile([P, NCOL], F32, name="bank2", tag="s2")
            nc.tensor.matmul_mx(out=bank2[:, 0:columns(u)], lhsT=woc[:].bitcast(FP8X4), lhsT_scale=wos[:],
                                rhs=qc[:].bitcast(FP8X4), rhs_scale=qs[:], start=True, stop=True)
            if kind in ("row0a", "row0b"):
                t0 = 0 if kind == "row0a" else HT
                empty(kind, ost[:, t0:t0 + HT, :], bank2[:].rearrange("p (f s) -> p f s", s=L))
                if kind == "row0b":
                    store(b, 0, TB, ost)
                return
            a0, c0 = BLOCKPAIRS[kind][0]
            if kind in ("dir1", "dir2"):
                empty(kind, ost[:, TB * a0:TB * (a0 + 1), TB * c0:TB * (c0 + 2)].rearrange("p f (e s) -> p f e s", e=2),
                      bank2[:].rearrange("p (e f s) -> p f e s", e=2, f=TB))
            elif kind in ("mir0", "mir1"):
                empty(kind, ost[:, TB * a0:TB * (a0 + 2), TB * c0:TB * (c0 + 1)].rearrange("p (e f) s -> p e f s", e=2),
                      bank2[:].rearrange("p (e s f) -> p e f s", e=2, s=TB))
            else:
                for e, (a, c) in enumerate(BLOCKPAIRS[kind]):
                    blk = bank2[:, BLK * e:BLK * (e + 1)]
                    view = blk.rearrange("p (f s) -> p f s", f=TB) if a <= c else blk.rearrange("p (s f) -> p f s", s=TB)
                    for h in range(2 if kind == "end2" else 1):
                        f0, f1 = (HT * h, HT * (h + 1)) if kind == "end2" else (0, TB)
                        empty(kind, ost[:, TB * a + f0:TB * a + f1, TB * c:TB * (c + 1)], view[:, f0:f1, :])
                        if kind == "end2":
                            store(b, TB * a + f0, TB * a + f1, ost)
            whole = (STORES if b else STORES0).get(kind)
            if whole is not None:
                store(b, TB * whole, TB * (whole + 1), ost)

        STORES = {"dir1": 1, "dir2": 2, "mix3": 3}
        STORES0 = {"mix1": 1, "dir2": 2, "mix3": 3}

        PIECES = tuple((P * t, P * (t + 1)) for t in range(T))
        xt0 = x_transpose(0)
        bps = ps1.tile([P, P], BF16, name="bps", tag="s1")
        nc.tensor.transpose(bps[:], brows[:], ident[:])
        for n0, n1 in PIECES[:2]:
            for w in (0, 2, 1):
                w_regroup(nc.scalar.copy, w, n0, n1)
        x_copy(0, xt0, 0, 1)
        job2 = p_mul(0, 2)
        x_copy(0, xt0, 1, 2)
        p_quant(job2)
        w_quant(0, *PIECES[0])
        quant_x(0)
        w_quant(1, *PIECES[0])
        x_four(0, 1)
        w_quant(2, *PIECES[0])
        x_tiles(0)
        x_outer(0, 1, 2)
        x_inner_blocks(0, 2, 4)
        nc.vector.tensor_copy(out=biasf[:], in_=bps[:, 0:8])
        for w in (0, 2, 1):
            w_quant(w, *PIECES[1])
        for piece in PIECES[2:]:
            for w in (0, 2, 1):
                w_regroup(nc.vector.tensor_copy, w, *piece)
            for w in (0, 2, 1):
                w_quant(w, *piece)
        job0 = p_mul(0, 0)
        x_inner_long(0)
        p_quant(job0)
        job1 = p_mul(0, 1)
        x_outer(0, 0, 1)
        x_inner_blocks(0, 1, 2)
        p_quant(job1)
        x_outer(0, 2, 4)
        wog = keep.tile([P, P, T], BF16, name="wog", align_bytes=64)

        PJOBS = {0: (0, 3), 3: (1, 0), 4: (1, 2), 5: (1, 1), 6: (1, 4)}
        PJOBS0 = {0: (0, 4), 2: (0, 3), 3: (1, 0), 4: (1, 2), 5: (1, 1), 6: (1, 4)}

        planes = {}
        codes = {}
        ostage = {}
        pending = []
        for s in range(NU + LAGD):
            u2 = s - LAGD
            if u2 >= 0:
                b2 = units[u2][0]
                if b2 not in ostage:
                    ostage[b2] = ring.tile([P, L, L], F32, name="ost", tag="ost")
                stage2(u2, codes[u2][0], codes[u2][1], ostage[b2])
            if s < NU:
                planes[s] = ring.tile([P, T, columns(s)], BF16, name="pl", tag="pl", bufs=5)
                if s == 1:
                    bias_terms(0)
                if s == 2 * UB - 2:
                    bias_terms(1)
                for t in range(T):
                    stage1(s, t, planes[s])
                if s == 1:
                    regroup(nc.scalar.copy, wog[:], woraw[:])
            u1 = s - 1
            if 0 <= u1 < NU:
                g2 = ring.tile([P, columns(u1), T], BF16, name="g2", tag="g2", align_bytes=64, bufs=3)
                regroup(nc.vector.tensor_copy, g2[:], planes[u1][:])
            for job in pending:
                p_quant(job)
            pending = []
            b, r = divmod(s, UB)
            table = PJOBS if b else PJOBS0
            if r in table and b + table[r][0] < B:
                pending.append(p_mul(b + table[r][0], table[r][1]))
            if s == 0:
                p_copy(0)
            if s == 2:
                nc.vector.quantize_mx(out=woc[:].bitcast(FP8X4), scales=wos[:], in_=wog[:].rearrange("p n t -> p (n t)"))
                x_copy(1, x_transpose(1), 2, 4)
            if s == 4:
                quant_x(1)
            if b + 1 < B:
                if r == 1:
                    x_tiles(b + 1)
                    if b < 2:
                        x_four(b + 1, b + 1)
                    x_inner_long(b + 1)
                if r == 2:
                    x_outer(b + 1)
                if r == 3:
                    x_inner_blocks(b + 1)
                if r == 7:
                    p_copy(b + 1)
            if 0 <= u1 < NU:
                qc = ring.tile([P, columns(u1)], U32, name="qc", tag="qc", align_bytes=64, bufs=LAGD + 2)
                qs = ring.tile([P, columns(u1)], U8, name="qs", tag="qs", align_bytes=64, bufs=LAGD + 2)
                nc.vector.quantize_mx(out=qc[:].bitcast(FP8X4), scales=qs[:], in_=g2[:].rearrange("p n t -> p (n t)"))
                codes[u1] = (qc, qs)
